import numpy as np
import ml_dtypes


def mxq(x, axis, fmt="e4m3"):
    dtype, down = {"e4m3": (ml_dtypes.float8_e4m3fn, 7), "e5m2": (ml_dtypes.float8_e5m2, 14)}[fmt]
    v = np.moveaxis(np.asarray(x, np.float32).astype(ml_dtypes.bfloat16).astype(np.float64), axis, -1)
    blocks = v.reshape(v.shape[:-1] + (-1, 32))
    amax = np.abs(blocks).max(-1, keepdims=True)
    byte = np.maximum(np.where(amax > 0, np.frexp(amax)[1] - 1 + 127, 0) - down, 1)
    scale = np.exp2(byte - 127.0)
    codes = (blocks / scale).astype(np.float32).astype(dtype).astype(np.float64)
    return np.moveaxis((codes * scale).reshape(v.shape), -1, axis)


WIDE = False


def mx_kscale(k):
    if not WIDE:
        return np.ones(k)
    levels = np.array([10, -10, 5, -5, 0])
    a = np.random.permutation(np.resize(levels, k // 512 * 4)).reshape(k // 512, 4)
    idx = np.arange(k)
    return np.exp2(a[idx // 512, idx % 128 // 32])


BF16 = ml_dtypes.bfloat16


def bf(x):
    return np.asarray(x, np.float32).astype(BF16)


def f64(x):
    return np.asarray(x).astype(np.float64)


E2M1 = np.array([0.0, 0.5, 1.0, 1.5, 2.0, 3.0, 4.0, 6.0, -0.0, -0.5, -1.0, -1.5, -2.0, -3.0, -4.0, -6.0])


def pack_weight(w, fmt):
    k, n = w.shape
    w = f64(bf(w)).reshape(k // 32, 32, n)
    amax = np.abs(w).max(1)
    if fmt == "e4m3":
        byte = np.frexp(amax)[1] - 1 + 127 - 7
    else:
        mant, ex = np.frexp(amax / 6.0)
        byte = np.where(mant > 0.5, ex, ex - 1) + 127
    byte = np.clip(np.where(amax > 0, byte, 1), 1, 254)
    scaled = (w * np.exp2(127.0 - byte)[:, None, :]).reshape(k, n).astype(np.float32)
    by_word = np.ascontiguousarray(scaled.reshape(k // 512, 128, 4, n).transpose(0, 1, 3, 2))
    if fmt == "e4m3":
        words = by_word.astype(ml_dtypes.float8_e4m3fn).view(np.uint8)
    else:
        c = by_word.astype(ml_dtypes.float4_e2m1fn).view(np.uint8) & 0xF
        words = c[..., 0::2] | (c[..., 1::2] << 4)
    return np.ascontiguousarray(words), np.ascontiguousarray(byte.astype(np.uint8).reshape(k // 512, 16, n))


def unpack_weight(words, scales, fmt):
    g, p, n, _ = words.shape
    if fmt == "e4m3":
        vals = np.ascontiguousarray(words).view(ml_dtypes.float8_e4m3fn).astype(np.float64)
    else:
        nib = np.empty((g, p, n, 4), np.uint8)
        nib[..., 0::2] = words & 0xF
        nib[..., 1::2] = words >> 4
        vals = E2M1[nib]
    vals = vals * np.repeat(np.exp2(scales.astype(np.float64) - 127.0), 8, axis=1)[..., None]
    return vals.transpose(0, 1, 3, 2).reshape(g * 512, n)


B, Lt, La, Dt, Da, H = 2, 512, 512, 1024, 1024, 1024
F = Dt + Da


def setup_inputs():
    u = mx_kscale(F)
    scores = bf(np.random.standard_normal((B, Lt, La)) * 3.0)
    auxiliary = bf(np.random.standard_normal((B, La, Da)) * u[Dt:])
    target = bf(np.random.standard_normal((B, Lt, Dt)) * u[:Dt])
    Wf_words, Wf_scales = pack_weight(np.random.standard_normal((F, Dt)) / np.sqrt(F) / u[:, None], "e4m3")
    b_f = bf(np.random.standard_normal(Dt) * 0.1)
    return {
        "scores": scores,
        "auxiliary": auxiliary,
        "target": target,
        "Wf_words": Wf_words,
        "Wf_scales": Wf_scales,
        "b_f": b_f,
    }


def reference(scores, auxiliary, target, Wf_words, Wf_scales, b_f):
    sc = f64(scores)
    e = np.exp(sc - sc.max(-1, keepdims=True))
    attn = e / e.sum(-1, keepdims=True)
    weighted_aux = mxq(attn, 2, "e4m3") @ mxq(f64(auxiliary), 1, "e4m3")
    x = np.concatenate([f64(target), weighted_aux], axis=-1)
    y = np.tanh((mxq(x, 2, "e4m3") @ unpack_weight(Wf_words, Wf_scales, "e4m3")) + f64(b_f))
    return y.transpose(0, 2, 1)

@@ -1,0 +1,214 @@
+from contextlib import ExitStack
+
+import concourse.mybir as mybir
+from concourse.masks import make_identity
+
+F32 = mybir.dt.float32
+BF16 = mybir.dt.bfloat16
+I32 = mybir.dt.int32
+U32 = mybir.dt.uint32
+U8 = mybir.dt.uint8
+FP8X4 = mybir.dt.float8_e4m3fn_x4
+ACT = mybir.ActivationFunctionType
+ALU = mybir.AluOpType
+AXIS = mybir.AxisListType
+
+P = 128
+PACK = 4
+K_PASS = P * PACK
+
+B = 2
+LT = 512
+LA = 512
+DT = 1024
+DA = 1024
+LT_TILES = LT // P
+TARGET_PASSES = DT // K_PASS
+AUX_PASSES = DA // K_PASS
+PASSES = TARGET_PASSES + AUX_PASSES
+OUT_TILES = DT // P
+
+FLOPS = 2 * B * LT * LA * DA + 2 * B * LT * (DT + DA) * DT
+
+
+def tile_informationfusion_pb_kernel(tc, scores, auxiliary, target, Wf_words, Wf_scales, b_f, out):
+    nc = tc.nc
+    with ExitStack() as ctx:
+        const = ctx.enter_context(tc.tile_pool(name="const", bufs=1))
+        per_batch = ctx.enter_context(tc.tile_pool(name="per_batch", bufs=B))
+        per_pass = ctx.enter_context(tc.tile_pool(name="per_pass", bufs=B * PASSES))
+        stats = ctx.enter_context(tc.tile_pool(name="stats", bufs=B * LT_TILES))
+        work = ctx.enter_context(tc.tile_pool(name="work", bufs=3))
+        results = ctx.enter_context(tc.tile_pool(name="results", bufs=4))
+        psum_flip = ctx.enter_context(tc.psum_pool(name="psum_flip", bufs=2))
+        psum_pool1 = ctx.enter_context(tc.psum_pool(name="psum_pool1", bufs=2))
+        psum_y = ctx.enter_context(tc.psum_pool(name="psum_y", bufs=4))
+
+        ident_bf16 = const.tile([P, P], BF16)
+        make_identity(nc, ident_bf16[:])
+        ident_f32 = const.tile([P, P], F32)
+        make_identity(nc, ident_f32[:])
+
+        w_planes = const.tile([P, DT], U8, align_bytes=64)
+        nc.vector.memset(w_planes[:].bitcast(I32), 0)
+        bias_rows = const.tile([P, P], BF16)
+        nc.vector.memset(bias_rows[:], 0.0)
+
+        scores_sb = []
+        aux_raw = []
+        target_raw = []
+
+        def load_batch(b):
+            s_tile = per_batch.tile([P, LT_TILES, LA], BF16)
+            for i in range(LT_TILES):
+                nc.sync.dma_start(out=s_tile[:, i, :], in_=scores[b, i * P : (i + 1) * P, :])
+            a_tile = per_batch.tile([P, PACK, DA], BF16)
+            nc.sync.dma_start(out=a_tile[:], in_=auxiliary[b].rearrange("(q j) d -> q j d", j=PACK))
+            t_tile = per_batch.tile([P, LT_TILES, DT], BF16)
+            nc.sync.dma_start(out=t_tile[:], in_=target[b].rearrange("(i p) k -> p i k", p=P))
+            scores_sb.append(s_tile)
+            aux_raw.append(a_tile)
+            target_raw.append(t_tile)
+
+        load_batch(0)
+        nc.scalar.dma_start(out=bias_rows[0:OUT_TILES, :], in_=b_f.rearrange("(m p) -> m p", p=P))
+        for quad in range(4):
+            nc.sync.dma_start(
+                out=w_planes[32 * quad : 32 * quad + 16, :].bitcast(I32),
+                in_=Wf_scales[:, 4 * quad : 4 * quad + 4, :].bitcast(I32),
+            )
+        w_codes = const.tile([P, PASSES, DT], U32, align_bytes=64)
+        for g in range(PASSES):
+            nc.sync.dma_start(
+                out=w_codes[:, g, :].bitcast(I32),
+                in_=Wf_words[g].rearrange("p n t -> p (n t)").bitcast(I32),
+            )
+        load_batch(1)
+
+        bias_flip = psum_flip.tile([P, P], BF16, tag="flip")
+        nc.tensor.transpose(out=bias_flip[:], in_=bias_rows[:], identity=ident_bf16[:])
+        bias_col = const.tile([P, OUT_TILES], F32)
+        nc.vector.tensor_copy(out=bias_col[:], in_=bias_flip[:, 0:OUT_TILES])
+
+        x_codes = {}
+        x_scales = {}
+
+        def quantise_x(b, g, x_grouped):
+            codes = per_pass.tile([P, LT], U32, align_bytes=64)
+            planes = per_pass.tile([P, LT], U8, align_bytes=64)
+            nc.vector.quantize_mx(
+                out=codes[:].bitcast(FP8X4),
+                scales=planes[:],
+                in_=x_grouped[:].rearrange("p r t -> p (r t)"),
+            )
+            x_codes[(b, g)] = codes
+            x_scales[(b, g)] = planes
+
+        def front(b):
+            attn_grouped = per_batch.tile([P, LT, PACK], BF16, align_bytes=64)
+            attn_codes = per_batch.tile([P, LT], U32, align_bytes=64)
+            attn_scales = per_batch.tile([P, LT], U8, align_bytes=64)
+            for i in range(LT_TILES):
+                rows = slice(i * P, (i + 1) * P)
+                neg_max = stats.tile([P, 1], F32)
+                nc.vector.tensor_reduce(
+                    out=neg_max[:], in_=scores_sb[b][:, i, :], axis=AXIS.X, op=ALU.max, negate=True
+                )
+                exp_sorted = work.tile([P, PACK, P], F32)
+                row_sum = stats.tile([P, 1], F32)
+                nc.scalar.activation(
+                    out=exp_sorted[:].rearrange("p j q -> p q j"),
+                    in_=scores_sb[b][:, i, :].rearrange("p (q j) -> p q j", j=PACK),
+                    func=ACT.Exp,
+                    bias=neg_max[:],
+                    scale=1.0,
+                    accum_out=row_sum[:],
+                )
+                inv_sum = stats.tile([P, 1], F32)
+                nc.vector.reciprocal(out=inv_sum[:], in_=row_sum[:])
+                attn_sorted = work.tile([P, PACK, P], BF16)
+                nc.vector.tensor_scalar(
+                    out=attn_sorted[:], in0=exp_sorted[:], scalar1=inv_sum[:], scalar2=None, op0=ALU.mult
+                )
+                attn_flip = psum_flip.tile([P, PACK, P], BF16, tag="flip")
+                for j in range(PACK):
+                    nc.tensor.transpose(out=attn_flip[:, j, :], in_=attn_sorted[:, j, :], identity=ident_bf16[:])
+                nc.vector.tensor_copy(out=attn_grouped[:, rows, :], in_=attn_flip[:].rearrange("q j r -> q r j"))
+                nc.vector.quantize_mx(
+                    out=attn_codes[:, rows].bitcast(FP8X4),
+                    scales=attn_scales[:, rows],
+                    in_=attn_grouped[:, rows, :].rearrange("q r j -> q (r j)"),
+                )
+
+            aux_grouped = per_batch.tile([P, AUX_PASSES, PACK, P, PACK], BF16, align_bytes=64)
+            aux_codes = per_batch.tile([P, AUX_PASSES, PACK, P], U32, align_bytes=64)
+            aux_scales = per_batch.tile([P, AUX_PASSES, PACK, P], U8, align_bytes=64)
+            for h in range(AUX_PASSES):
+                nc.vector.tensor_copy(
+                    out=aux_grouped[:, h].rearrange("q t p j -> q p j t"),
+                    in_=aux_raw[b][:, :, h * K_PASS : (h + 1) * K_PASS].rearrange("q j (p t) -> q p j t", t=PACK),
+                )
+                nc.vector.quantize_mx(
+                    out=aux_codes[:, h].rearrange("q t p -> q (t p)").bitcast(FP8X4),
+                    scales=aux_scales[:, h].rearrange("q t p -> q (t p)"),
+                    in_=aux_grouped[:, h].rearrange("q t p j -> q (t p j)"),
+                )
+
+            target_words = target_raw[b][:].bitcast(F32)
+            for g in range(TARGET_PASSES):
+                x_grouped = per_pass.tile([P, LT, PACK], BF16, align_bytes=64)
+                for half in range(LT_TILES // 2):
+                    target_flip = psum_flip.tile([P, 2, 2 * P], F32, tag="flip")
+                    for u in range(2):
+                        for s in range(2):
+                            nc.tensor.transpose(
+                                out=target_flip[:, u, s * P : (s + 1) * P],
+                                in_=target_words[:, 2 * half + s, 256 * g + u : 256 * (g + 1) : 2],
+                                identity=ident_f32[:],
+                            )
+                    nc.scalar.copy(
+                        out=x_grouped[:, 2 * half * P : 2 * (half + 1) * P, :].bitcast(F32),
+                        in_=target_flip[:].rearrange("p u r -> p r u"),
+                    )
+                quantise_x(b, g, x_grouped)
+
+            for h in range(AUX_PASSES):
+                x_grouped = per_pass.tile([P, LT, PACK], BF16, align_bytes=64)
+                for i in range(LT_TILES):
+                    rows = slice(i * P, (i + 1) * P)
+                    pooled = psum_pool1.tile([P, PACK, P], F32)
+                    for t in range(PACK):
+                        nc.tensor.matmul_mx(
+                            out=pooled[:, t, :],
+                            lhsT=aux_codes[:, h, t, :].bitcast(FP8X4),
+                            lhsT_scale=aux_scales[:, h, t, :],
+                            rhs=attn_codes[:, rows].bitcast(FP8X4),
+                            rhs_scale=attn_scales[:, rows],
+                            start=True,
+                            stop=True,
+                        )
+                    nc.scalar.copy(out=x_grouped[:, rows, :], in_=pooled[:].rearrange("p t r -> p r t"))
+                quantise_x(b, TARGET_PASSES + h, x_grouped)
+
+        def fuse(b):
+            for m in range(OUT_TILES):
+                cols = slice(m * P, (m + 1) * P)
+                y_acc = psum_y.tile([P, LT], F32)
+                for g in range(PASSES):
+                    nc.tensor.matmul_mx(
+                        out=y_acc[:],
+                        lhsT=w_codes[:, g, cols].bitcast(FP8X4),
+                        lhsT_scale=w_planes[4 * g : P, cols],
+                        rhs=x_codes[(b, g)][:].bitcast(FP8X4),
+                        rhs_scale=x_scales[(b, g)][:],
+                        start=(g == 0),
+                        stop=(g == PASSES - 1),
+                    )
+                y_sb = results.tile([P, LT], F32)
+                nc.scalar.activation(out=y_sb[:], in_=y_acc[:], func=ACT.Tanh, bias=bias_col[:, m : m + 1], scale=1.0)
+                nc.sync.dma_start(out=out[b, cols, :], in_=y_sb[:])
+
+        front(0)
+        front(1)
+        fuse(0)
+        fuse(1)

@@ -27,6 +27,8 @@ TARGET_PASSES = DT // K_PASS
 AUX_PASSES = DA // K_PASS
 PASSES = TARGET_PASSES + AUX_PASSES
 OUT_TILES = DT // P
+FRONT_BANKS = 4
+OUT_BANKS = 4
 
 FLOPS = 2 * B * LT * LA * DA + 2 * B * LT * (DT + DA) * DT
 
@@ -34,15 +36,15 @@ FLOPS = 2 * B * LT * LA * DA + 2 * B * LT * (DT + DA) * DT
 def tile_informationfusion_pb_kernel(tc, scores, auxiliary, target, Wf_words, Wf_scales, b_f, out):
     nc = tc.nc
     with ExitStack() as ctx:
+        ctx.enter_context(tc.manual_schedule())
         const = ctx.enter_context(tc.tile_pool(name="const", bufs=1))
         per_batch = ctx.enter_context(tc.tile_pool(name="per_batch", bufs=B))
         per_pass = ctx.enter_context(tc.tile_pool(name="per_pass", bufs=B * PASSES))
-        stats = ctx.enter_context(tc.tile_pool(name="stats", bufs=B * LT_TILES))
-        work = ctx.enter_context(tc.tile_pool(name="work", bufs=3))
-        results = ctx.enter_context(tc.tile_pool(name="results", bufs=4))
-        psum_flip = ctx.enter_context(tc.psum_pool(name="psum_flip", bufs=2))
-        psum_pool1 = ctx.enter_context(tc.psum_pool(name="psum_pool1", bufs=2))
-        psum_y = ctx.enter_context(tc.psum_pool(name="psum_y", bufs=4))
+        per_tile = ctx.enter_context(tc.tile_pool(name="per_tile", bufs=B * LT_TILES))
+        work = ctx.enter_context(tc.tile_pool(name="work", bufs=LT_TILES))
+        results = ctx.enter_context(tc.tile_pool(name="results", bufs=OUT_BANKS))
+        psum_front = ctx.enter_context(tc.psum_pool(name="psum_front", bufs=FRONT_BANKS))
+        psum_out = ctx.enter_context(tc.psum_pool(name="psum_out", bufs=OUT_BANKS))
 
         ident_bf16 = const.tile([P, P], BF16)
         make_identity(nc, ident_bf16[:])
@@ -53,162 +55,290 @@ def tile_informationfusion_pb_kernel(tc, scores, auxiliary, target, Wf_words, Wf
         nc.vector.memset(w_planes[:].bitcast(I32), 0)
         bias_rows = const.tile([P, P], BF16)
         nc.vector.memset(bias_rows[:], 0.0)
+        nc.scalar.dma_start(out=bias_rows[0:OUT_TILES, :], in_=b_f.rearrange("(m p) -> m p", p=P))
+
+        table_warmer = const.tile([P, 1], F32)
+        nc.vector.memset(table_warmer[:], 0.0)
+        nc.scalar.activation(out=table_warmer[:], in_=table_warmer[:], func=ACT.Exp)
 
         scores_sb = []
         aux_raw = []
         target_raw = []
-
-        def load_batch(b):
+        for b in range(B):
             s_tile = per_batch.tile([P, LT_TILES, LA], BF16)
-            for i in range(LT_TILES):
-                nc.sync.dma_start(out=s_tile[:, i, :], in_=scores[b, i * P : (i + 1) * P, :])
             a_tile = per_batch.tile([P, PACK, DA], BF16)
-            nc.sync.dma_start(out=a_tile[:], in_=auxiliary[b].rearrange("(q j) d -> q j d", j=PACK))
             t_tile = per_batch.tile([P, LT_TILES, DT], BF16)
-            nc.sync.dma_start(out=t_tile[:], in_=target[b].rearrange("(i p) k -> p i k", p=P))
             scores_sb.append(s_tile)
             aux_raw.append(a_tile)
             target_raw.append(t_tile)
-
-        load_batch(0)
-        nc.scalar.dma_start(out=bias_rows[0:OUT_TILES, :], in_=b_f.rearrange("(m p) -> m p", p=P))
-        for quad in range(4):
-            nc.sync.dma_start(
-                out=w_planes[32 * quad : 32 * quad + 16, :].bitcast(I32),
-                in_=Wf_scales[:, 4 * quad : 4 * quad + 4, :].bitcast(I32),
-            )
         w_codes = const.tile([P, PASSES, DT], U32, align_bytes=64)
-        for g in range(PASSES):
+
+        def load_scores(b):
+            for i in range(LT_TILES):
+                nc.sync.dma_start(out=scores_sb[b][:, i, :], in_=scores[b, i * P : (i + 1) * P, :])
+
+        def load_auxiliary(b):
+            nc.sync.dma_start(out=aux_raw[b][:], in_=auxiliary[b].rearrange("(q j) d -> q j d", j=PACK))
+
+        def load_target(b):
+            nc.sync.dma_start(out=target_raw[b][:], in_=target[b].rearrange("(i p) k -> p i k", p=P))
+
+        def load_weight_scales():
+            for quad in range(4):
+                nc.sync.dma_start(
+                    out=w_planes[32 * quad : 32 * quad + 16, :].bitcast(I32),
+                    in_=Wf_scales[:, 4 * quad : 4 * quad + 4, :].bitcast(I32),
+                )
+
+        def load_weight_pass(g):
             nc.sync.dma_start(
                 out=w_codes[:, g, :].bitcast(I32),
                 in_=Wf_words[g].rearrange("p n t -> p (n t)").bitcast(I32),
             )
-        load_batch(1)
 
-        bias_flip = psum_flip.tile([P, P], BF16, tag="flip")
+        load_scores(0)
+        load_auxiliary(0)
+        load_target(0)
+        load_weight_scales()
+        for g in range(TARGET_PASSES):
+            load_weight_pass(g)
+        load_scores(1)
+        load_target(1)
+        for g in range(TARGET_PASSES, PASSES):
+            load_weight_pass(g)
+        load_auxiliary(1)
+
+        attn_grouped = []
+        attn_codes = []
+        attn_scales = []
+        aux_grouped = []
+        aux_codes = []
+        aux_scales = []
+        x_grouped = {}
+        x_codes = {}
+        x_scales = {}
+        for b in range(B):
+            at_grouped = per_batch.tile([P, LT, PACK], BF16, align_bytes=64)
+            at_codes = per_batch.tile([P, LT], U32, align_bytes=64)
+            at_scales = per_batch.tile([P, LT], U8, align_bytes=64)
+            ax_grouped = per_batch.tile([P, AUX_PASSES, PACK, P, PACK], BF16, align_bytes=64)
+            ax_codes = per_batch.tile([P, AUX_PASSES, PACK, P], U32, align_bytes=64)
+            ax_scales = per_batch.tile([P, AUX_PASSES, PACK, P], U8, align_bytes=64)
+            attn_grouped.append(at_grouped)
+            attn_codes.append(at_codes)
+            attn_scales.append(at_scales)
+            aux_grouped.append(ax_grouped)
+            aux_codes.append(ax_codes)
+            aux_scales.append(ax_scales)
+            for g in range(PASSES):
+                xg_tile = per_pass.tile([P, LT, PACK], BF16, align_bytes=64)
+                xc_tile = per_pass.tile([P, LT], U32, align_bytes=64)
+                xs_tile = per_pass.tile([P, LT], U8, align_bytes=64)
+                x_grouped[(b, g)] = xg_tile
+                x_codes[(b, g)] = xc_tile
+                x_scales[(b, g)] = xs_tile
+
+        neg_max = {}
+        row_sum = {}
+        exp_sorted = {}
+        attn_sorted = {}
+        y_acc = {}
+
+        def row_max(b, i):
+            neg_max[(b, i)] = per_tile.tile([P, 1], F32, name="neg_max")
+            nc.vector.tensor_reduce(
+                out=neg_max[(b, i)][:], in_=scores_sb[b][:, i, :], axis=AXIS.X, op=ALU.max, negate=True
+            )
+
+        def exponentials(b, i):
+            exp_sorted[(b, i)] = work.tile([P, PACK, P], F32, name="exp_sorted")
+            row_sum[(b, i)] = per_tile.tile([P, 1], F32, name="row_sum")
+            nc.scalar.activation(
+                out=exp_sorted[(b, i)][:].rearrange("p j q -> p q j"),
+                in_=scores_sb[b][:, i, :].rearrange("p (q j) -> p q j", j=PACK),
+                func=ACT.Exp,
+                bias=neg_max[(b, i)][:],
+                scale=1.0,
+                accum_out=row_sum[(b, i)][:],
+            )
+
+        def normalise(b, i):
+            inv_sum = per_tile.tile([P, 1], F32)
+            nc.vector.reciprocal(out=inv_sum[:], in_=row_sum[(b, i)][:])
+            attn_sorted[(b, i)] = work.tile([P, PACK, P], BF16, name="attn_sorted")
+            nc.vector.tensor_scalar(
+                out=attn_sorted[(b, i)][:], in0=exp_sorted[(b, i)][:], scalar1=inv_sum[:], scalar2=None, op0=ALU.mult
+            )
+
+        def flip_attn(b, i):
+            rows = slice(i * P, (i + 1) * P)
+            attn_flip = psum_front.tile([P, PACK, P], BF16, tag="front")
+            for j in range(PACK):
+                nc.tensor.transpose(out=attn_flip[:, j, :], in_=attn_sorted[(b, i)][:, j, :], identity=ident_bf16[:])
+            nc.scalar.copy(out=attn_grouped[b][:, rows, :], in_=attn_flip[:].rearrange("q j r -> q r j"))
+
+        def quantise_attn(b, i):
+            rows = slice(i * P, (i + 1) * P)
+            nc.vector.quantize_mx(
+                out=attn_codes[b][:, rows].bitcast(FP8X4),
+                scales=attn_scales[b][:, rows],
+                in_=attn_grouped[b][:, rows, :].rearrange("q r j -> q (r j)"),
+            )
+
+        def regroup_aux(b, h):
+            nc.vector.tensor_copy(
+                out=aux_grouped[b][:, h].rearrange("q t p j -> q p j t"),
+                in_=aux_raw[b][:, :, h * K_PASS : (h + 1) * K_PASS].rearrange("q j (p t) -> q p j t", t=PACK),
+            )
+
+        def quantise_aux(b, h):
+            nc.vector.quantize_mx(
+                out=aux_codes[b][:, h].rearrange("q t p -> q (t p)").bitcast(FP8X4),
+                scales=aux_scales[b][:, h].rearrange("q t p -> q (t p)"),
+                in_=aux_grouped[b][:, h].rearrange("q t p j -> q (t p j)"),
+            )
+
+        def flip_target(b, g, half):
+            target_words = target_raw[b][:].bitcast(F32)
+            target_flip = psum_front.tile([P, 2, 2 * P], F32, tag="front")
+            for u in range(2):
+                for s in range(2):
+                    nc.tensor.transpose(
+                        out=target_flip[:, u, s * P : (s + 1) * P],
+                        in_=target_words[:, 2 * half + s, 256 * g + u : 256 * (g + 1) : 2],
+                        identity=ident_f32[:],
+                    )
+            nc.scalar.copy(
+                out=x_grouped[(b, g)][:, 2 * half * P : 2 * (half + 1) * P, :].bitcast(F32),
+                in_=target_flip[:].rearrange("p u r -> p r u"),
+            )
+
+        def quantise_x(b, g):
+            nc.vector.quantize_mx(
+                out=x_codes[(b, g)][:].bitcast(FP8X4),
+                scales=x_scales[(b, g)][:],
+                in_=x_grouped[(b, g)][:].rearrange("p r t -> p (r t)"),
+            )
+
+        def pool(b, h, i):
+            rows = slice(i * P, (i + 1) * P)
+            pooled = psum_front.tile([P, PACK, P], F32, tag="front")
+            for t in range(PACK):
+                nc.tensor.matmul_mx(
+                    out=pooled[:, t, :],
+                    lhsT=aux_codes[b][:, h, t, :].bitcast(FP8X4),
+                    lhsT_scale=aux_scales[b][:, h, t, :],
+                    rhs=attn_codes[b][:, rows].bitcast(FP8X4),
+                    rhs_scale=attn_scales[b][:, rows],
+                    start=True,
+                    stop=True,
+                )
+            grouped = x_grouped[(b, TARGET_PASSES + h)][:, rows, :]
+            if h == 0:
+                nc.scalar.copy(out=grouped, in_=pooled[:].rearrange("p t r -> p r t"))
+            else:
+                nc.vector.tensor_copy(out=grouped, in_=pooled[:].rearrange("p t r -> p r t"))
+
+        def fuse(b, m, passes):
+            cols = slice(m * P, (m + 1) * P)
+            for g in passes:
+                if g == 0:
+                    y_acc[(b, m)] = psum_out.tile([P, LT], F32, name="y_acc")
+                nc.tensor.matmul_mx(
+                    out=y_acc[(b, m)][:],
+                    lhsT=w_codes[:, g, cols].bitcast(FP8X4),
+                    lhsT_scale=w_planes[4 * g : P, cols],
+                    rhs=x_codes[(b, g)][:].bitcast(FP8X4),
+                    rhs_scale=x_scales[(b, g)][:],
+                    start=(g == 0),
+                    stop=(g == PASSES - 1),
+                )
+
+        def finish(b, m):
+            y_sb = results.tile([P, LT], F32)
+            nc.scalar.activation(
+                out=y_sb[:], in_=y_acc[(b, m)][:], func=ACT.Tanh, bias=bias_col[:, m : m + 1], scale=1.0
+            )
+            nc.sync.dma_start(out=out[b, m * P : (m + 1) * P, :], in_=y_sb[:])
+
+        target_passes = range(TARGET_PASSES)
+        aux_passes = range(TARGET_PASSES, PASSES)
+        all_passes = range(PASSES)
+        early_tiles = range(OUT_BANKS)
+        late_tiles = range(OUT_BANKS, OUT_TILES)
+
+        for i in range(LT_TILES):
+            row_max(0, i)
+            exponentials(0, i)
+        for h in range(AUX_PASSES):
+            for i in (2 * h, 2 * h + 1):
+                normalise(0, i)
+                flip_attn(0, i)
+            regroup_aux(0, h)
+        for h in range(AUX_PASSES):
+            quantise_aux(0, h)
+        for i in range(LT_TILES):
+            quantise_attn(0, i)
+        for g in target_passes:
+            for half in range(2):
+                flip_target(0, g, half)
+        bias_flip = psum_front.tile([P, P], BF16, tag="front")
         nc.tensor.transpose(out=bias_flip[:], in_=bias_rows[:], identity=ident_bf16[:])
         bias_col = const.tile([P, OUT_TILES], F32)
         nc.vector.tensor_copy(out=bias_col[:], in_=bias_flip[:, 0:OUT_TILES])
-
-        x_codes = {}
-        x_scales = {}
-
-        def quantise_x(b, g, x_grouped):
-            codes = per_pass.tile([P, LT], U32, align_bytes=64)
-            planes = per_pass.tile([P, LT], U8, align_bytes=64)
-            nc.vector.quantize_mx(
-                out=codes[:].bitcast(FP8X4),
-                scales=planes[:],
-                in_=x_grouped[:].rearrange("p r t -> p (r t)"),
-            )
-            x_codes[(b, g)] = codes
-            x_scales[(b, g)] = planes
-
-        def front(b):
-            attn_grouped = per_batch.tile([P, LT, PACK], BF16, align_bytes=64)
-            attn_codes = per_batch.tile([P, LT], U32, align_bytes=64)
-            attn_scales = per_batch.tile([P, LT], U8, align_bytes=64)
+        for g in target_passes:
+            quantise_x(0, g)
+            row_max(1, g)
+        for h in range(AUX_PASSES):
             for i in range(LT_TILES):
-                rows = slice(i * P, (i + 1) * P)
-                neg_max = stats.tile([P, 1], F32)
-                nc.vector.tensor_reduce(
-                    out=neg_max[:], in_=scores_sb[b][:, i, :], axis=AXIS.X, op=ALU.max, negate=True
-                )
-                exp_sorted = work.tile([P, PACK, P], F32)
-                row_sum = stats.tile([P, 1], F32)
-                nc.scalar.activation(
-                    out=exp_sorted[:].rearrange("p j q -> p q j"),
-                    in_=scores_sb[b][:, i, :].rearrange("p (q j) -> p q j", j=PACK),
-                    func=ACT.Exp,
-                    bias=neg_max[:],
-                    scale=1.0,
-                    accum_out=row_sum[:],
-                )
-                inv_sum = stats.tile([P, 1], F32)
-                nc.vector.reciprocal(out=inv_sum[:], in_=row_sum[:])
-                attn_sorted = work.tile([P, PACK, P], BF16)
-                nc.vector.tensor_scalar(
-                    out=attn_sorted[:], in0=exp_sorted[:], scalar1=inv_sum[:], scalar2=None, op0=ALU.mult
-                )
-                attn_flip = psum_flip.tile([P, PACK, P], BF16, tag="flip")
-                for j in range(PACK):
-                    nc.tensor.transpose(out=attn_flip[:, j, :], in_=attn_sorted[:, j, :], identity=ident_bf16[:])
-                nc.vector.tensor_copy(out=attn_grouped[:, rows, :], in_=attn_flip[:].rearrange("q j r -> q r j"))
-                nc.vector.quantize_mx(
-                    out=attn_codes[:, rows].bitcast(FP8X4),
-                    scales=attn_scales[:, rows],
-                    in_=attn_grouped[:, rows, :].rearrange("q r j -> q (r j)"),
-                )
+                pool(0, h, i)
+            for m in early_tiles:
+                fuse(0, m, [h])
+        for g in aux_passes:
+            quantise_x(0, g)
 
-            aux_grouped = per_batch.tile([P, AUX_PASSES, PACK, P, PACK], BF16, align_bytes=64)
-            aux_codes = per_batch.tile([P, AUX_PASSES, PACK, P], U32, align_bytes=64)
-            aux_scales = per_batch.tile([P, AUX_PASSES, PACK, P], U8, align_bytes=64)
-            for h in range(AUX_PASSES):
-                nc.vector.tensor_copy(
-                    out=aux_grouped[:, h].rearrange("q t p j -> q p j t"),
-                    in_=aux_raw[b][:, :, h * K_PASS : (h + 1) * K_PASS].rearrange("q j (p t) -> q p j t", t=PACK),
-                )
-                nc.vector.quantize_mx(
-                    out=aux_codes[:, h].rearrange("q t p -> q (t p)").bitcast(FP8X4),
-                    scales=aux_scales[:, h].rearrange("q t p -> q (t p)"),
-                    in_=aux_grouped[:, h].rearrange("q t p j -> q (t p j)"),
-                )
+        for i in (0, 1):
+            exponentials(1, i)
+        for g in target_passes:
+            for half in range(2):
+                flip_target(1, g, half)
+        for i in (2, 3):
+            row_max(1, i)
+            exponentials(1, i)
+        for h in range(AUX_PASSES):
+            for m in (2 * h, 2 * h + 1):
+                fuse(0, m, aux_passes)
+            for i in (2 * h, 2 * h + 1):
+                normalise(1, i)
+                flip_attn(1, i)
+            for m in (2 * h, 2 * h + 1):
+                finish(0, m)
+            regroup_aux(1, h)
+        for h in range(AUX_PASSES):
+            quantise_aux(1, h)
+        for i in range(LT_TILES):
+            quantise_attn(1, i)
+        for g in target_passes:
+            quantise_x(1, g)
+        fuse(0, 4, all_passes)
+        finish(0, 4)
+        fuse(0, 5, all_passes)
+        for half in range(2):
+            for i in (2 * half, 2 * half + 1):
+                for h in range(AUX_PASSES):
+                    pool(1, h, i)
+            finish(0, 5 + half)
+            fuse(0, 6 + half, all_passes)
+        finish(0, 7)
+        for g in aux_passes:
+            quantise_x(1, g)
 
-            target_words = target_raw[b][:].bitcast(F32)
-            for g in range(TARGET_PASSES):
-                x_grouped = per_pass.tile([P, LT, PACK], BF16, align_bytes=64)
-                for half in range(LT_TILES // 2):
-                    target_flip = psum_flip.tile([P, 2, 2 * P], F32, tag="flip")
-                    for u in range(2):
-                        for s in range(2):
-                            nc.tensor.transpose(
-                                out=target_flip[:, u, s * P : (s + 1) * P],
-                                in_=target_words[:, 2 * half + s, 256 * g + u : 256 * (g + 1) : 2],
-                                identity=ident_f32[:],
-                            )
-                    nc.scalar.copy(
-                        out=x_grouped[:, 2 * half * P : 2 * (half + 1) * P, :].bitcast(F32),
-                        in_=target_flip[:].rearrange("p u r -> p r u"),
-                    )
-                quantise_x(b, g, x_grouped)
-
-            for h in range(AUX_PASSES):
-                x_grouped = per_pass.tile([P, LT, PACK], BF16, align_bytes=64)
-                for i in range(LT_TILES):
-                    rows = slice(i * P, (i + 1) * P)
-                    pooled = psum_pool1.tile([P, PACK, P], F32)
-                    for t in range(PACK):
-                        nc.tensor.matmul_mx(
-                            out=pooled[:, t, :],
-                            lhsT=aux_codes[:, h, t, :].bitcast(FP8X4),
-                            lhsT_scale=aux_scales[:, h, t, :],
-                            rhs=attn_codes[:, rows].bitcast(FP8X4),
-                            rhs_scale=attn_scales[:, rows],
-                            start=True,
-                            stop=True,
-                        )
-                    nc.scalar.copy(out=x_grouped[:, rows, :], in_=pooled[:].rearrange("p t r -> p r t"))
-                quantise_x(b, TARGET_PASSES + h, x_grouped)
-
-        def fuse(b):
-            for m in range(OUT_TILES):
-                cols = slice(m * P, (m + 1) * P)
-                y_acc = psum_y.tile([P, LT], F32)
-                for g in range(PASSES):
-                    nc.tensor.matmul_mx(
-                        out=y_acc[:],
-                        lhsT=w_codes[:, g, cols].bitcast(FP8X4),
-                        lhsT_scale=w_planes[4 * g : P, cols],
-                        rhs=x_codes[(b, g)][:].bitcast(FP8X4),
-                        rhs_scale=x_scales[(b, g)][:],
-                        start=(g == 0),
-                        stop=(g == PASSES - 1),
-                    )
-                y_sb = results.tile([P, LT], F32)
-                nc.scalar.activation(out=y_sb[:], in_=y_acc[:], func=ACT.Tanh, bias=bias_col[:, m : m + 1], scale=1.0)
-                nc.sync.dma_start(out=out[b, cols, :], in_=y_sb[:])
-
-        front(0)
-        front(1)
-        fuse(0)
-        fuse(1)
+        for g in target_passes:
+            for m in early_tiles:
+                fuse(1, m, [g])
+        for m in early_tiles:
+            fuse(1, m, aux_passes)
+            finish(1, m)
+        for m in late_tiles:
+            fuse(1, m, all_passes)
+            finish(1, m)

@@ -36,7 +36,6 @@ FLOPS = 2 * B * LT * LA * DA + 2 * B * LT * (DT + DA) * DT
 def tile_informationfusion_pb_kernel(tc, scores, auxiliary, target, Wf_words, Wf_scales, b_f, out):
     nc = tc.nc
     with ExitStack() as ctx:
-        ctx.enter_context(tc.manual_schedule())
         const = ctx.enter_context(tc.tile_pool(name="const", bufs=1))
         per_batch = ctx.enter_context(tc.tile_pool(name="per_batch", bufs=B))
         per_pass = ctx.enter_context(tc.tile_pool(name="per_pass", bufs=B * PASSES))
@@ -270,15 +269,13 @@ def tile_informationfusion_pb_kernel(tc, scores, auxiliary, target, Wf_words, Wf
         for i in range(LT_TILES):
             row_max(0, i)
             exponentials(0, i)
-        for h in range(AUX_PASSES):
-            for i in (2 * h, 2 * h + 1):
-                normalise(0, i)
-                flip_attn(0, i)
-            regroup_aux(0, h)
-        for h in range(AUX_PASSES):
-            quantise_aux(0, h)
+        for i in range(LT_TILES):
+            normalise(0, i)
+            flip_attn(0, i)
+        regroup_aux(0, 0)
         for i in range(LT_TILES):
             quantise_attn(0, i)
+        quantise_aux(0, 0)
         for g in target_passes:
             for half in range(2):
                 flip_target(0, g, half)
@@ -286,19 +283,24 @@ def tile_informationfusion_pb_kernel(tc, scores, auxiliary, target, Wf_words, Wf
         nc.tensor.transpose(out=bias_flip[:], in_=bias_rows[:], identity=ident_bf16[:])
         bias_col = const.tile([P, OUT_TILES], F32)
         nc.vector.tensor_copy(out=bias_col[:], in_=bias_flip[:, 0:OUT_TILES])
-        for g in target_passes:
-            quantise_x(0, g)
-            row_max(1, g)
-        for h in range(AUX_PASSES):
-            for i in range(LT_TILES):
-                pool(0, h, i)
-            for m in early_tiles:
-                fuse(0, m, [h])
+        for i in range(LT_TILES):
+            pool(0, 0, i)
+        regroup_aux(0, 1)
+        quantise_x(0, 0)
+        quantise_aux(0, 1)
+        quantise_x(0, 1)
+        for m in early_tiles:
+            fuse(0, m, [0])
+        for i in (0, 1):
+            row_max(1, i)
+            exponentials(1, i)
+        for i in range(LT_TILES):
+            pool(0, 1, i)
+        for m in early_tiles:
+            fuse(0, m, [1])
         for g in aux_passes:
             quantise_x(0, g)
 
-        for i in (0, 1):
-            exponentials(1, i)
         for g in target_passes:
             for half in range(2):
                 flip_target(1, g, half)

@@ -11,11 +11,14 @@ U8 = mybir.dt.uint8
 FP8X4 = mybir.dt.float8_e4m3fn_x4
 ACT = mybir.ActivationFunctionType
 ALU = mybir.AluOpType
-AXIS = mybir.AxisListType
 
 P = 128
 PACK = 4
 K_PASS = P * PACK
+PAIRS_IN_WORD = 2
+QUADRANTS = 4
+QUADRANT = P // QUADRANTS
+SCALE_ROWS = 4
 
 B = 2
 LT = 512
@@ -29,6 +32,9 @@ PASSES = TARGET_PASSES + AUX_PASSES
 OUT_TILES = DT // P
 FRONT_BANKS = 4
 OUT_BANKS = 4
+FLIP_TILES = 2
+STEPS = 2
+assert LT_TILES == 2 * STEPS and OUT_BANKS == 2 * STEPS and AUX_PASSES == STEPS and OUT_TILES == 2 * OUT_BANKS
 
 FLOPS = 2 * B * LT * LA * DA + 2 * B * LT * (DT + DA) * DT
 
@@ -36,6 +42,7 @@ FLOPS = 2 * B * LT * LA * DA + 2 * B * LT * (DT + DA) * DT
 def tile_informationfusion_pb_kernel(tc, scores, auxiliary, target, Wf_words, Wf_scales, b_f, out):
     nc = tc.nc
     with ExitStack() as ctx:
+        ctx.enter_context(tc.manual_schedule())
         const = ctx.enter_context(tc.tile_pool(name="const", bufs=1))
         per_batch = ctx.enter_context(tc.tile_pool(name="per_batch", bufs=B))
         per_pass = ctx.enter_context(tc.tile_pool(name="per_pass", bufs=B * PASSES))
@@ -83,10 +90,11 @@ def tile_informationfusion_pb_kernel(tc, scores, auxiliary, target, Wf_words, Wf
             nc.sync.dma_start(out=target_raw[b][:], in_=target[b].rearrange("(i p) k -> p i k", p=P))
 
         def load_weight_scales():
-            for quad in range(4):
+            for quad in range(QUADRANTS):
+                first = QUADRANT * quad
                 nc.sync.dma_start(
-                    out=w_planes[32 * quad : 32 * quad + 16, :].bitcast(I32),
-                    in_=Wf_scales[:, 4 * quad : 4 * quad + 4, :].bitcast(I32),
+                    out=w_planes[first : first + PASSES * SCALE_ROWS, :].bitcast(I32),
+                    in_=Wf_scales[:, SCALE_ROWS * quad : SCALE_ROWS * (quad + 1), :].bitcast(I32),
                 )
 
         def load_weight_pass(g):
@@ -144,9 +152,16 @@ def tile_informationfusion_pb_kernel(tc, scores, auxiliary, target, Wf_words, Wf
         y_acc = {}
 
         def row_max(b, i):
+            negated = work.tile([P, LA], BF16)
             neg_max[(b, i)] = per_tile.tile([P, 1], F32, name="neg_max")
-            nc.vector.tensor_reduce(
-                out=neg_max[(b, i)][:], in_=scores_sb[b][:, i, :], axis=AXIS.X, op=ALU.max, negate=True
+            nc.vector.tensor_scalar(
+                out=negated[:],
+                in0=scores_sb[b][:, i, :],
+                scalar1=-1.0,
+                scalar2=None,
+                op0=ALU.mult,
+                op1=ALU.min,
+                accum_out=neg_max[(b, i)][:],
             )
 
         def exponentials(b, i):
@@ -197,18 +212,22 @@ def tile_informationfusion_pb_kernel(tc, scores, auxiliary, target, Wf_words, Wf
                 in_=aux_grouped[b][:, h].rearrange("q t p j -> q (t p j)"),
             )
 
-        def flip_target(b, g, half):
-            target_words = target_raw[b][:].bitcast(F32)
-            target_flip = psum_front.tile([P, 2, 2 * P], F32, tag="front")
-            for u in range(2):
-                for s in range(2):
+        def flip_target(b, g, part):
+            pairs_in_pass = P * PAIRS_IN_WORD
+            target_pairs = target_raw[b][:].bitcast(F32)
+            target_flip = psum_front.tile([P, PAIRS_IN_WORD, FLIP_TILES * P], F32, tag="front")
+            for u in range(PAIRS_IN_WORD):
+                for s in range(FLIP_TILES):
                     nc.tensor.transpose(
                         out=target_flip[:, u, s * P : (s + 1) * P],
-                        in_=target_words[:, 2 * half + s, 256 * g + u : 256 * (g + 1) : 2],
+                        in_=target_pairs[
+                            :, FLIP_TILES * part + s, pairs_in_pass * g + u : pairs_in_pass * (g + 1) : PAIRS_IN_WORD
+                        ],
                         identity=ident_f32[:],
                     )
+            rows = slice(FLIP_TILES * part * P, FLIP_TILES * (part + 1) * P)
             nc.scalar.copy(
-                out=x_grouped[(b, g)][:, 2 * half * P : 2 * (half + 1) * P, :].bitcast(F32),
+                out=x_grouped[(b, g)][:, rows, :].bitcast(F32),
                 in_=target_flip[:].rearrange("p u r -> p r u"),
             )
 
@@ -246,7 +265,7 @@ def tile_informationfusion_pb_kernel(tc, scores, auxiliary, target, Wf_words, Wf
                 nc.tensor.matmul_mx(
                     out=y_acc[(b, m)][:],
                     lhsT=w_codes[:, g, cols].bitcast(FP8X4),
-                    lhsT_scale=w_planes[4 * g : P, cols],
+                    lhsT_scale=w_planes[SCALE_ROWS * g : P, cols],
                     rhs=x_codes[(b, g)][:].bitcast(FP8X4),
                     rhs_scale=x_scales[(b, g)][:],
                     start=(g == 0),
@@ -265,6 +284,8 @@ def tile_informationfusion_pb_kernel(tc, scores, auxiliary, target, Wf_words, Wf
         all_passes = range(PASSES)
         early_tiles = range(OUT_BANKS)
         late_tiles = range(OUT_BANKS, OUT_TILES)
+        first_lt_tiles = range(LT_TILES // 2)
+        last_lt_tiles = range(LT_TILES // 2, LT_TILES)
 
         for i in range(LT_TILES):
             row_max(0, i)
@@ -277,8 +298,8 @@ def tile_informationfusion_pb_kernel(tc, scores, auxiliary, target, Wf_words, Wf
             quantise_attn(0, i)
         quantise_aux(0, 0)
         for g in target_passes:
-            for half in range(2):
-                flip_target(0, g, half)
+            for part in range(LT_TILES // FLIP_TILES):
+                flip_target(0, g, part)
         bias_flip = psum_front.tile([P, P], BF16, tag="front")
         nc.tensor.transpose(out=bias_flip[:], in_=bias_rows[:], identity=ident_bf16[:])
         bias_col = const.tile([P, OUT_TILES], F32)
@@ -291,7 +312,7 @@ def tile_informationfusion_pb_kernel(tc, scores, auxiliary, target, Wf_words, Wf
         quantise_x(0, 1)
         for m in early_tiles:
             fuse(0, m, [0])
-        for i in (0, 1):
+        for i in first_lt_tiles:
             row_max(1, i)
             exponentials(1, i)
         for i in range(LT_TILES):
@@ -302,36 +323,40 @@ def tile_informationfusion_pb_kernel(tc, scores, auxiliary, target, Wf_words, Wf
             quantise_x(0, g)
 
         for g in target_passes:
-            for half in range(2):
-                flip_target(1, g, half)
-        for i in (2, 3):
+            for part in range(LT_TILES // FLIP_TILES):
+                flip_target(1, g, part)
+        for i in last_lt_tiles:
             row_max(1, i)
             exponentials(1, i)
-        for h in range(AUX_PASSES):
-            for m in (2 * h, 2 * h + 1):
+        for step in range(STEPS):
+            two = (2 * step, 2 * step + 1)
+            for m in two:
                 fuse(0, m, aux_passes)
-            for i in (2 * h, 2 * h + 1):
+            for i in two:
                 normalise(1, i)
                 flip_attn(1, i)
-            for m in (2 * h, 2 * h + 1):
+            for m in two:
                 finish(0, m)
-            regroup_aux(1, h)
+            regroup_aux(1, step)
         for h in range(AUX_PASSES):
             quantise_aux(1, h)
         for i in range(LT_TILES):
             quantise_attn(1, i)
         for g in target_passes:
             quantise_x(1, g)
-        fuse(0, 4, all_passes)
-        finish(0, 4)
-        fuse(0, 5, all_passes)
-        for half in range(2):
-            for i in (2 * half, 2 * half + 1):
+        m = late_tiles[0]
+        fuse(0, m, all_passes)
+        finish(0, m)
+        for step in range(STEPS):
+            m += 1
+            fuse(0, m, all_passes)
+            for i in (2 * step, 2 * step + 1):
                 for h in range(AUX_PASSES):
                     pool(1, h, i)
-            finish(0, 5 + half)
-            fuse(0, 6 + half, all_passes)
-        finish(0, 7)
+            finish(0, m)
+        m += 1
+        fuse(0, m, all_passes)
+        finish(0, m)
         for g in aux_passes:
             quantise_x(1, g)
 

@@ -15,7 +15,8 @@ ALU = mybir.AluOpType
 P = 128
 PACK = 4
 K_PASS = P * PACK
-PAIRS_IN_WORD = 2
+PAIRS = 2
+PAIR = 2
 QUADRANTS = 4
 QUADRANT = P // QUADRANTS
 SCALE_ROWS = 4
@@ -25,16 +26,19 @@ LT = 512
 LA = 512
 DT = 1024
 DA = 1024
-LT_TILES = LT // P
+CHUNK = 256
+TILES = CHUNK // P
+CHUNKS_IN_BATCH = LT // CHUNK
+CHUNKS = B * CHUNKS_IN_BATCH
 TARGET_PASSES = DT // K_PASS
 AUX_PASSES = DA // K_PASS
 PASSES = TARGET_PASSES + AUX_PASSES
 OUT_TILES = DT // P
+WEIGHT_HALVES = 2
+TILES_IN_HALF = OUT_TILES // WEIGHT_HALVES
+STORE_TILES = 2
 FRONT_BANKS = 4
 OUT_BANKS = 4
-FLIP_TILES = 2
-STEPS = 2
-assert LT_TILES == 2 * STEPS and OUT_BANKS == 2 * STEPS and AUX_PASSES == STEPS and OUT_TILES == 2 * OUT_BANKS
 
 FLOPS = 2 * B * LT * LA * DA + 2 * B * LT * (DT + DA) * DT
 
@@ -45,49 +49,68 @@ def tile_informationfusion_pb_kernel(tc, scores, auxiliary, target, Wf_words, Wf
         ctx.enter_context(tc.manual_schedule())
         const = ctx.enter_context(tc.tile_pool(name="const", bufs=1))
         per_batch = ctx.enter_context(tc.tile_pool(name="per_batch", bufs=B))
-        per_pass = ctx.enter_context(tc.tile_pool(name="per_pass", bufs=B * PASSES))
-        per_tile = ctx.enter_context(tc.tile_pool(name="per_tile", bufs=B * LT_TILES))
-        work = ctx.enter_context(tc.tile_pool(name="work", bufs=LT_TILES))
-        results = ctx.enter_context(tc.tile_pool(name="results", bufs=OUT_BANKS))
+        per_chunk = ctx.enter_context(tc.tile_pool(name="per_chunk", bufs=CHUNKS))
+        per_half = ctx.enter_context(tc.tile_pool(name="per_half", bufs=B * AUX_PASSES))
+        per_weight_half = ctx.enter_context(tc.tile_pool(name="per_weight_half", bufs=WEIGHT_HALVES))
+        per_pass = ctx.enter_context(tc.tile_pool(name="per_pass", bufs=CHUNKS * PASSES))
+        per_tile = ctx.enter_context(tc.tile_pool(name="per_tile", bufs=CHUNKS * TILES))
+        work = ctx.enter_context(tc.tile_pool(name="work", bufs=2 * TILES))
+        results = ctx.enter_context(tc.tile_pool(name="results", bufs=OUT_TILES))
         psum_front = ctx.enter_context(tc.psum_pool(name="psum_front", bufs=FRONT_BANKS))
         psum_out = ctx.enter_context(tc.psum_pool(name="psum_out", bufs=OUT_BANKS))
 
-        ident_bf16 = const.tile([P, P], BF16)
-        make_identity(nc, ident_bf16[:])
         ident_f32 = const.tile([P, P], F32)
         make_identity(nc, ident_f32[:])
+        ident_bf16 = const.tile([P, P], BF16)
+        make_identity(nc, ident_bf16[:])
 
         w_planes = const.tile([P, DT], U8, align_bytes=64)
-        nc.vector.memset(w_planes[:].bitcast(I32), 0)
         bias_rows = const.tile([P, P], BF16)
         nc.vector.memset(bias_rows[:], 0.0)
         nc.scalar.dma_start(out=bias_rows[0:OUT_TILES, :], in_=b_f.rearrange("(m p) -> m p", p=P))
+        nc.vector.memset(w_planes[:].bitcast(I32), 0)
 
         table_warmer = const.tile([P, 1], F32)
         nc.vector.memset(table_warmer[:], 0.0)
         nc.scalar.activation(out=table_warmer[:], in_=table_warmer[:], func=ACT.Exp)
 
         scores_sb = []
-        aux_raw = []
         target_raw = []
-        for b in range(B):
-            s_tile = per_batch.tile([P, LT_TILES, LA], BF16)
-            a_tile = per_batch.tile([P, PACK, DA], BF16)
-            t_tile = per_batch.tile([P, LT_TILES, DT], BF16)
+        aux_raw = {}
+        for c in range(CHUNKS):
+            s_tile = per_chunk.tile([P, TILES, LA], BF16)
             scores_sb.append(s_tile)
-            aux_raw.append(a_tile)
+            t_tile = per_chunk.tile([P, TILES, DT], BF16)
             target_raw.append(t_tile)
-        w_codes = const.tile([P, PASSES, DT], U32, align_bytes=64)
+        for b in range(B):
+            for h in range(AUX_PASSES):
+                aux_raw[(b, h)] = per_half.tile([P, PACK, K_PASS], BF16, name="aux_raw")
+        w_codes = []
+        for half in range(WEIGHT_HALVES):
+            w_tile = per_weight_half.tile([P, PASSES, DT // WEIGHT_HALVES], U32, align_bytes=64)
+            w_codes.append(w_tile)
 
-        def load_scores(b):
-            for i in range(LT_TILES):
-                nc.sync.dma_start(out=scores_sb[b][:, i, :], in_=scores[b, i * P : (i + 1) * P, :])
+        def chunk_rows(c):
+            first = (c % CHUNKS_IN_BATCH) * CHUNK
+            return slice(first, first + CHUNK)
 
-        def load_auxiliary(b):
-            nc.sync.dma_start(out=aux_raw[b][:], in_=auxiliary[b].rearrange("(q j) d -> q j d", j=PACK))
+        def load_scores(c):
+            nc.sync.dma_start(
+                out=scores_sb[c][:],
+                in_=scores[c // CHUNKS_IN_BATCH, chunk_rows(c), :].rearrange("(i p) a -> p i a", p=P),
+            )
 
-        def load_target(b):
-            nc.sync.dma_start(out=target_raw[b][:], in_=target[b].rearrange("(i p) k -> p i k", p=P))
+        def load_target(c):
+            nc.sync.dma_start(
+                out=target_raw[c][:],
+                in_=target[c // CHUNKS_IN_BATCH, chunk_rows(c), :].rearrange("(i p) k -> p i k", p=P),
+            )
+
+        def load_auxiliary(b, h):
+            cols = slice(h * K_PASS, (h + 1) * K_PASS)
+            nc.sync.dma_start(
+                out=aux_raw[(b, h)][:], in_=auxiliary[b].rearrange("(q j) d -> q j d", j=PACK)[:, :, cols]
+            )
 
         def load_weight_scales():
             for quad in range(QUADRANTS):
@@ -97,112 +120,130 @@ def tile_informationfusion_pb_kernel(tc, scores, auxiliary, target, Wf_words, Wf
                     in_=Wf_scales[:, SCALE_ROWS * quad : SCALE_ROWS * (quad + 1), :].bitcast(I32),
                 )
 
-        def load_weight_pass(g):
+        def load_weight_half(half):
+            cols = slice(half * DT // WEIGHT_HALVES, (half + 1) * DT // WEIGHT_HALVES)
             nc.sync.dma_start(
-                out=w_codes[:, g, :].bitcast(I32),
-                in_=Wf_words[g].rearrange("p n t -> p (n t)").bitcast(I32),
+                out=w_codes[half][:].bitcast(I32),
+                in_=Wf_words.rearrange("g p n t -> p g (n t)").bitcast(I32)[:, :, cols],
             )
 
         load_scores(0)
-        load_auxiliary(0)
+        load_auxiliary(0, 0)
+        load_auxiliary(0, 1)
         load_target(0)
         load_weight_scales()
-        for g in range(TARGET_PASSES):
-            load_weight_pass(g)
+        load_weight_half(0)
         load_scores(1)
         load_target(1)
-        for g in range(TARGET_PASSES, PASSES):
-            load_weight_pass(g)
-        load_auxiliary(1)
+        load_weight_half(1)
+        load_scores(2)
+        load_auxiliary(1, 0)
+        load_auxiliary(1, 1)
+        load_target(2)
+        load_scores(3)
+        load_target(3)
 
         attn_grouped = []
         attn_codes = []
         attn_scales = []
-        aux_grouped = []
-        aux_codes = []
-        aux_scales = []
         x_grouped = {}
         x_codes = {}
         x_scales = {}
-        for b in range(B):
-            at_grouped = per_batch.tile([P, LT, PACK], BF16, align_bytes=64)
-            at_codes = per_batch.tile([P, LT], U32, align_bytes=64)
-            at_scales = per_batch.tile([P, LT], U8, align_bytes=64)
-            ax_grouped = per_batch.tile([P, AUX_PASSES, PACK, P, PACK], BF16, align_bytes=64)
-            ax_codes = per_batch.tile([P, AUX_PASSES, PACK, P], U32, align_bytes=64)
-            ax_scales = per_batch.tile([P, AUX_PASSES, PACK, P], U8, align_bytes=64)
+        for c in range(CHUNKS):
+            at_grouped = per_chunk.tile([P, CHUNK, PACK], BF16, align_bytes=64)
+            at_codes = per_chunk.tile([P, CHUNK], U32, align_bytes=64)
+            at_scales = per_chunk.tile([P, CHUNK], U8, align_bytes=64)
             attn_grouped.append(at_grouped)
             attn_codes.append(at_codes)
             attn_scales.append(at_scales)
+            for g in range(PASSES):
+                xg_tile = per_pass.tile([P, CHUNK, PACK], BF16, align_bytes=64)
+                xc_tile = per_pass.tile([P, CHUNK], U32, align_bytes=64)
+                xs_tile = per_pass.tile([P, CHUNK], U8, align_bytes=64)
+                x_grouped[(c, g)] = xg_tile
+                x_codes[(c, g)] = xc_tile
+                x_scales[(c, g)] = xs_tile
+        aux_grouped = []
+        aux_codes = []
+        aux_scales = []
+        for b in range(B):
+            ax_grouped = per_batch.tile([P, AUX_PASSES, PACK, P, PACK], BF16, align_bytes=64)
+            ax_codes = per_batch.tile([P, AUX_PASSES, PACK, P], U32, align_bytes=64)
+            ax_scales = per_batch.tile([P, AUX_PASSES, PACK, P], U8, align_bytes=64)
             aux_grouped.append(ax_grouped)
             aux_codes.append(ax_codes)
             aux_scales.append(ax_scales)
-            for g in range(PASSES):
-                xg_tile = per_pass.tile([P, LT, PACK], BF16, align_bytes=64)
-                xc_tile = per_pass.tile([P, LT], U32, align_bytes=64)
-                xs_tile = per_pass.tile([P, LT], U8, align_bytes=64)
-                x_grouped[(b, g)] = xg_tile
-                x_codes[(b, g)] = xc_tile
-                x_scales[(b, g)] = xs_tile
 
         neg_max = {}
         row_sum = {}
         exp_sorted = {}
         attn_sorted = {}
         y_acc = {}
+        y_pair = {}
 
-        def row_max(b, i):
-            negated = work.tile([P, LA], BF16)
-            neg_max[(b, i)] = per_tile.tile([P, 1], F32, name="neg_max")
-            nc.vector.tensor_scalar(
-                out=negated[:],
-                in0=scores_sb[b][:, i, :],
-                scalar1=-1.0,
-                scalar2=None,
-                op0=ALU.mult,
-                op1=ALU.min,
-                accum_out=neg_max[(b, i)][:],
-            )
+        def row_max(c):
+            for i in range(TILES):
+                negated = work.tile([P, LA], BF16)
+                neg_max[(c, i)] = per_tile.tile([P, 1], F32, name="neg_max")
+                nc.vector.tensor_scalar(
+                    out=negated[:],
+                    in0=scores_sb[c][:, i, :],
+                    scalar1=-1.0,
+                    scalar2=None,
+                    op0=ALU.mult,
+                    op1=ALU.min,
+                    accum_out=neg_max[(c, i)][:],
+                )
 
-        def exponentials(b, i):
-            exp_sorted[(b, i)] = work.tile([P, PACK, P], F32, name="exp_sorted")
-            row_sum[(b, i)] = per_tile.tile([P, 1], F32, name="row_sum")
-            nc.scalar.activation(
-                out=exp_sorted[(b, i)][:].rearrange("p j q -> p q j"),
-                in_=scores_sb[b][:, i, :].rearrange("p (q j) -> p q j", j=PACK),
-                func=ACT.Exp,
-                bias=neg_max[(b, i)][:],
-                scale=1.0,
-                accum_out=row_sum[(b, i)][:],
-            )
+        def exponentials(c):
+            row_sum[c] = per_chunk.tile([P, TILES], F32, name="row_sum")
+            for i in range(TILES):
+                exp_sorted[(c, i)] = work.tile([P, PAIRS, P, PAIR], F32, name="exp_sorted")
+                nc.scalar.activation(
+                    out=exp_sorted[(c, i)][:].rearrange("p u q e -> p q u e"),
+                    in_=scores_sb[c][:, i, :].rearrange("p (q u e) -> p q u e", u=PAIRS, e=PAIR),
+                    func=ACT.Exp,
+                    bias=neg_max[(c, i)][:],
+                    scale=1.0,
+                    accum_out=row_sum[c][:, i : i + 1],
+                )
 
-        def normalise(b, i):
-            inv_sum = per_tile.tile([P, 1], F32)
-            nc.vector.reciprocal(out=inv_sum[:], in_=row_sum[(b, i)][:])
-            attn_sorted[(b, i)] = work.tile([P, PACK, P], BF16, name="attn_sorted")
-            nc.vector.tensor_scalar(
-                out=attn_sorted[(b, i)][:], in0=exp_sorted[(b, i)][:], scalar1=inv_sum[:], scalar2=None, op0=ALU.mult
-            )
+        def normalise(c):
+            inv_sum = per_chunk.tile([P, TILES], F32)
+            nc.vector.reciprocal(out=inv_sum[:], in_=row_sum[c][:])
+            for i in range(TILES):
+                attn_sorted[(c, i)] = work.tile([P, LA], BF16, name="attn_sorted")
+                nc.vector.tensor_scalar(
+                    out=attn_sorted[(c, i)][:],
+                    in0=exp_sorted[(c, i)][:].rearrange("p u q e -> p (u q e)"),
+                    scalar1=inv_sum[:, i : i + 1],
+                    scalar2=None,
+                    op0=ALU.mult,
+                )
 
-        def flip_attn(b, i):
-            rows = slice(i * P, (i + 1) * P)
-            attn_flip = psum_front.tile([P, PACK, P], BF16, tag="front")
-            for j in range(PACK):
-                nc.tensor.transpose(out=attn_flip[:, j, :], in_=attn_sorted[(b, i)][:, j, :], identity=ident_bf16[:])
-            nc.scalar.copy(out=attn_grouped[b][:, rows, :], in_=attn_flip[:].rearrange("q j r -> q r j"))
+        def flip_attn(c):
+            attn_flip = psum_front.tile([P, PAIRS, CHUNK], F32, tag="front")
+            for i in range(TILES):
+                attn_pairs = attn_sorted[(c, i)][:].bitcast(F32)
+                for u in range(PAIRS):
+                    nc.tensor.transpose(
+                        out=attn_flip[:, u, i * P : (i + 1) * P],
+                        in_=attn_pairs[:, u * P : (u + 1) * P],
+                        identity=ident_f32[:],
+                    )
+            nc.scalar.copy(out=attn_grouped[c][:].bitcast(F32), in_=attn_flip[:].rearrange("q u r -> q r u"))
 
-        def quantise_attn(b, i):
-            rows = slice(i * P, (i + 1) * P)
+        def quantise_attn(c):
             nc.vector.quantize_mx(
-                out=attn_codes[b][:, rows].bitcast(FP8X4),
-                scales=attn_scales[b][:, rows],
-                in_=attn_grouped[b][:, rows, :].rearrange("q r j -> q (r j)"),
+                out=attn_codes[c][:].bitcast(FP8X4),
+                scales=attn_scales[c][:],
+                in_=attn_grouped[c][:].rearrange("q r j -> q (r j)"),
             )
 
         def regroup_aux(b, h):
             nc.vector.tensor_copy(
                 out=aux_grouped[b][:, h].rearrange("q t p j -> q p j t"),
-                in_=aux_raw[b][:, :, h * K_PASS : (h + 1) * K_PASS].rearrange("q j (p t) -> q p j t", t=PACK),
+                in_=aux_raw[(b, h)][:].rearrange("q j (p t) -> q p j t", t=PACK),
             )
 
         def quantise_aux(b, h):
@@ -212,33 +253,28 @@ def tile_informationfusion_pb_kernel(tc, scores, auxiliary, target, Wf_words, Wf
                 in_=aux_grouped[b][:, h].rearrange("q t p j -> q (t p j)"),
             )
 
-        def flip_target(b, g, part):
-            pairs_in_pass = P * PAIRS_IN_WORD
-            target_pairs = target_raw[b][:].bitcast(F32)
-            target_flip = psum_front.tile([P, PAIRS_IN_WORD, FLIP_TILES * P], F32, tag="front")
-            for u in range(PAIRS_IN_WORD):
-                for s in range(FLIP_TILES):
+        def flip_target(c, g):
+            pairs_in_pass = P * PAIRS
+            target_pairs = target_raw[c][:].bitcast(F32)
+            target_flip = psum_front.tile([P, PAIRS, CHUNK], F32, tag="front")
+            for u in range(PAIRS):
+                for i in range(TILES):
                     nc.tensor.transpose(
-                        out=target_flip[:, u, s * P : (s + 1) * P],
-                        in_=target_pairs[
-                            :, FLIP_TILES * part + s, pairs_in_pass * g + u : pairs_in_pass * (g + 1) : PAIRS_IN_WORD
-                        ],
+                        out=target_flip[:, u, i * P : (i + 1) * P],
+                        in_=target_pairs[:, i, pairs_in_pass * g + u : pairs_in_pass * (g + 1) : PAIRS],
                         identity=ident_f32[:],
                     )
-            rows = slice(FLIP_TILES * part * P, FLIP_TILES * (part + 1) * P)
-            nc.scalar.copy(
-                out=x_grouped[(b, g)][:, rows, :].bitcast(F32),
-                in_=target_flip[:].rearrange("p u r -> p r u"),
-            )
+            nc.scalar.copy(out=x_grouped[(c, g)][:].bitcast(F32), in_=target_flip[:].rearrange("p u r -> p r u"))
 
-        def quantise_x(b, g):
+        def quantise_x(c, g):
             nc.vector.quantize_mx(
-                out=x_codes[(b, g)][:].bitcast(FP8X4),
-                scales=x_scales[(b, g)][:],
-                in_=x_grouped[(b, g)][:].rearrange("p r t -> p (r t)"),
+                out=x_codes[(c, g)][:].bitcast(FP8X4),
+                scales=x_scales[(c, g)][:],
+                in_=x_grouped[(c, g)][:].rearrange("p r t -> p (r t)"),
             )
 
-        def pool(b, h, i):
+        def pool(c, h, i):
+            b = c // CHUNKS_IN_BATCH
             rows = slice(i * P, (i + 1) * P)
             pooled = psum_front.tile([P, PACK, P], F32, tag="front")
             for t in range(PACK):
@@ -246,126 +282,124 @@ def tile_informationfusion_pb_kernel(tc, scores, auxiliary, target, Wf_words, Wf
                     out=pooled[:, t, :],
                     lhsT=aux_codes[b][:, h, t, :].bitcast(FP8X4),
                     lhsT_scale=aux_scales[b][:, h, t, :],
-                    rhs=attn_codes[b][:, rows].bitcast(FP8X4),
-                    rhs_scale=attn_scales[b][:, rows],
+                    rhs=attn_codes[c][:, rows].bitcast(FP8X4),
+                    rhs_scale=attn_scales[c][:, rows],
                     start=True,
                     stop=True,
                 )
-            grouped = x_grouped[(b, TARGET_PASSES + h)][:, rows, :]
+            grouped = x_grouped[(c, TARGET_PASSES + h)][:, rows, :]
             if h == 0:
                 nc.scalar.copy(out=grouped, in_=pooled[:].rearrange("p t r -> p r t"))
             else:
                 nc.vector.tensor_copy(out=grouped, in_=pooled[:].rearrange("p t r -> p r t"))
 
-        def fuse(b, m, passes):
+        def fuse(c, m, passes):
             cols = slice(m * P, (m + 1) * P)
+            half_cols = slice((m % TILES_IN_HALF) * P, (m % TILES_IN_HALF + 1) * P)
             for g in passes:
                 if g == 0:
-                    y_acc[(b, m)] = psum_out.tile([P, LT], F32, name="y_acc")
+                    y_acc[(c, m)] = psum_out.tile([P, CHUNK], F32, name="y_acc")
                 nc.tensor.matmul_mx(
-                    out=y_acc[(b, m)][:],
-                    lhsT=w_codes[:, g, cols].bitcast(FP8X4),
+                    out=y_acc[(c, m)][:],
+                    lhsT=w_codes[m // TILES_IN_HALF][:, g, half_cols].bitcast(FP8X4),
                     lhsT_scale=w_planes[SCALE_ROWS * g : P, cols],
-                    rhs=x_codes[(b, g)][:].bitcast(FP8X4),
-                    rhs_scale=x_scales[(b, g)][:],
+                    rhs=x_codes[(c, g)][:].bitcast(FP8X4),
+                    rhs_scale=x_scales[(c, g)][:],
                     start=(g == 0),
                     stop=(g == PASSES - 1),
                 )
 
-        def finish(b, m):
-            y_sb = results.tile([P, LT], F32)
+        def finish(c, m):
+            slot = m % STORE_TILES
+            if slot == 0:
+                y_pair[c] = results.tile([P, STORE_TILES, CHUNK], F32, name="y_pair")
             nc.scalar.activation(
-                out=y_sb[:], in_=y_acc[(b, m)][:], func=ACT.Tanh, bias=bias_col[:, m : m + 1], scale=1.0
+                out=y_pair[c][:, slot, :], in_=y_acc[(c, m)][:], func=ACT.Tanh, bias=bias_col[:, m : m + 1], scale=1.0
             )
-            nc.sync.dma_start(out=out[b, m * P : (m + 1) * P, :], in_=y_sb[:])
+            if slot == STORE_TILES - 1:
+                features = slice((m + 1 - STORE_TILES) * P, (m + 1) * P)
+                nc.sync.dma_start(
+                    out=out[c // CHUNKS_IN_BATCH, features, chunk_rows(c)].rearrange("(s p) r -> p s r", p=P),
+                    in_=y_pair[c][:],
+                )
 
         target_passes = range(TARGET_PASSES)
         aux_passes = range(TARGET_PASSES, PASSES)
         all_passes = range(PASSES)
         early_tiles = range(OUT_BANKS)
         late_tiles = range(OUT_BANKS, OUT_TILES)
-        first_lt_tiles = range(LT_TILES // 2)
-        last_lt_tiles = range(LT_TILES // 2, LT_TILES)
 
-        for i in range(LT_TILES):
-            row_max(0, i)
-            exponentials(0, i)
-        for i in range(LT_TILES):
-            normalise(0, i)
-            flip_attn(0, i)
+        def flip(c):
+            flip_attn(c)
+            for g in target_passes:
+                flip_target(c, g)
+
+        row_max(0)
+        exponentials(0)
         regroup_aux(0, 0)
-        for i in range(LT_TILES):
-            quantise_attn(0, i)
-        quantise_aux(0, 0)
-        for g in target_passes:
-            for part in range(LT_TILES // FLIP_TILES):
-                flip_target(0, g, part)
+        normalise(0)
+        flip(0)
         bias_flip = psum_front.tile([P, P], BF16, tag="front")
         nc.tensor.transpose(out=bias_flip[:], in_=bias_rows[:], identity=ident_bf16[:])
         bias_col = const.tile([P, OUT_TILES], F32)
-        nc.vector.tensor_copy(out=bias_col[:], in_=bias_flip[:, 0:OUT_TILES])
-        for i in range(LT_TILES):
-            pool(0, 0, i)
+        quantise_aux(0, 0)
         regroup_aux(0, 1)
-        quantise_x(0, 0)
+        quantise_attn(0)
         quantise_aux(0, 1)
-        quantise_x(0, 1)
-        for m in early_tiles:
-            fuse(0, m, [0])
-        for i in first_lt_tiles:
-            row_max(1, i)
-            exponentials(1, i)
-        for i in range(LT_TILES):
-            pool(0, 1, i)
-        for m in early_tiles:
-            fuse(0, m, [1])
+        for g in target_passes:
+            quantise_x(0, g)
+        nc.vector.tensor_copy(out=bias_col[:], in_=bias_flip[:, 0:OUT_TILES])
+        row_max(1)
+        for h in range(AUX_PASSES):
+            for i in range(TILES):
+                pool(0, h, i)
+        exponentials(1)
         for g in aux_passes:
             quantise_x(0, g)
+        normalise(1)
 
-        for g in target_passes:
-            for part in range(LT_TILES // FLIP_TILES):
-                flip_target(1, g, part)
-        for i in last_lt_tiles:
-            row_max(1, i)
-            exponentials(1, i)
-        for step in range(STEPS):
-            two = (2 * step, 2 * step + 1)
-            for m in two:
-                fuse(0, m, aux_passes)
-            for i in two:
-                normalise(1, i)
-                flip_attn(1, i)
-            for m in two:
-                finish(0, m)
-            regroup_aux(1, step)
-        for h in range(AUX_PASSES):
-            quantise_aux(1, h)
-        for i in range(LT_TILES):
-            quantise_attn(1, i)
-        for g in target_passes:
-            quantise_x(1, g)
-        m = late_tiles[0]
-        fuse(0, m, all_passes)
-        finish(0, m)
-        for step in range(STEPS):
-            m += 1
-            fuse(0, m, all_passes)
-            for i in (2 * step, 2 * step + 1):
-                for h in range(AUX_PASSES):
-                    pool(1, h, i)
-            finish(0, m)
-        m += 1
-        fuse(0, m, all_passes)
-        finish(0, m)
-        for g in aux_passes:
-            quantise_x(1, g)
-
-        for g in target_passes:
+        for c in range(CHUNKS):
+            nxt = c + 1
+            far = c + 2
             for m in early_tiles:
-                fuse(1, m, [g])
-        for m in early_tiles:
-            fuse(1, m, aux_passes)
-            finish(1, m)
-        for m in late_tiles:
-            fuse(1, m, all_passes)
-            finish(1, m)
+                fuse(c, m, target_passes)
+            if far < CHUNKS:
+                row_max(far)
+            for m in early_tiles:
+                fuse(c, m, aux_passes)
+                finish(c, m)
+            if c == 0:
+                flip(1)
+            if nxt < CHUNKS:
+                quantise_attn(nxt)
+                for g in target_passes:
+                    quantise_x(nxt, g)
+            if far < CHUNKS:
+                exponentials(far)
+            if c < AUX_PASSES:
+                regroup_aux(1, c)
+            for m in late_tiles[:2]:
+                fuse(c, m, all_passes)
+                finish(c, m)
+            if far >= CHUNKS and nxt < CHUNKS:
+                for h in range(AUX_PASSES):
+                    for i in range(TILES):
+                        pool(nxt, h, i)
+                for g in aux_passes:
+                    quantise_x(nxt, g)
+            for m in late_tiles[2:]:
+                fuse(c, m, all_passes)
+                finish(c, m)
+            if c == 1:
+                quantise_aux(1, 0)
+                quantise_aux(1, 1)
+            if far < CHUNKS:
+                normalise(far)
+            if far < CHUNKS:
+                for h in range(AUX_PASSES):
+                    for i in range(TILES):
+                        pool(nxt, h, i)
+                for g in aux_passes:
+                    quantise_x(nxt, g)
+            if far < CHUNKS:
+                flip(far)

@@ -35,7 +35,7 @@ AUX_PASSES = DA // K_PASS
 PASSES = TARGET_PASSES + AUX_PASSES
 OUT_TILES = DT // P
 WEIGHT_HALVES = 2
-TILES_IN_HALF = OUT_TILES // WEIGHT_HALVES
+PASSES_IN_HALF = PASSES // WEIGHT_HALVES
 STORE_TILES = 2
 FRONT_BANKS = 4
 OUT_BANKS = 4
@@ -59,15 +59,15 @@ def tile_informationfusion_pb_kernel(tc, scores, auxiliary, target, Wf_words, Wf
         psum_front = ctx.enter_context(tc.psum_pool(name="psum_front", bufs=FRONT_BANKS))
         psum_out = ctx.enter_context(tc.psum_pool(name="psum_out", bufs=OUT_BANKS))
 
+        bias_rows = const.tile([P, P], BF16)
+        nc.gpsimd.memset(bias_rows[:], 0.0)
+        nc.gpsimd.dma_start(out=bias_rows[0:OUT_TILES, :], in_=b_f.rearrange("(m p) -> m p", p=P))
         ident_f32 = const.tile([P, P], F32)
         make_identity(nc, ident_f32[:])
         ident_bf16 = const.tile([P, P], BF16)
         make_identity(nc, ident_bf16[:])
 
         w_planes = const.tile([P, DT], U8, align_bytes=64)
-        bias_rows = const.tile([P, P], BF16)
-        nc.vector.memset(bias_rows[:], 0.0)
-        nc.scalar.dma_start(out=bias_rows[0:OUT_TILES, :], in_=b_f.rearrange("(m p) -> m p", p=P))
         nc.vector.memset(w_planes[:].bitcast(I32), 0)
 
         table_warmer = const.tile([P, 1], F32)
@@ -87,7 +87,7 @@ def tile_informationfusion_pb_kernel(tc, scores, auxiliary, target, Wf_words, Wf
                 aux_raw[(b, h)] = per_half.tile([P, PACK, K_PASS], BF16, name="aux_raw")
         w_codes = []
         for half in range(WEIGHT_HALVES):
-            w_tile = per_weight_half.tile([P, PASSES, DT // WEIGHT_HALVES], U32, align_bytes=64)
+            w_tile = per_weight_half.tile([P, PASSES_IN_HALF, DT], U32, align_bytes=64)
             w_codes.append(w_tile)
 
         def chunk_rows(c):
@@ -97,13 +97,13 @@ def tile_informationfusion_pb_kernel(tc, scores, auxiliary, target, Wf_words, Wf
         def load_scores(c):
             nc.sync.dma_start(
                 out=scores_sb[c][:],
-                in_=scores[c // CHUNKS_IN_BATCH, chunk_rows(c), :].rearrange("(i p) a -> p i a", p=P),
+                in_=scores[c // CHUNKS_IN_BATCH, chunk_rows(c), :].rearrange("(p i) a -> p i a", i=TILES),
             )
 
         def load_target(c):
             nc.sync.dma_start(
                 out=target_raw[c][:],
-                in_=target[c // CHUNKS_IN_BATCH, chunk_rows(c), :].rearrange("(i p) k -> p i k", p=P),
+                in_=target[c // CHUNKS_IN_BATCH, chunk_rows(c), :].rearrange("(p i) k -> p i k", i=TILES),
             )
 
         def load_auxiliary(b, h):
@@ -121,21 +121,21 @@ def tile_informationfusion_pb_kernel(tc, scores, auxiliary, target, Wf_words, Wf
                 )
 
         def load_weight_half(half):
-            cols = slice(half * DT // WEIGHT_HALVES, (half + 1) * DT // WEIGHT_HALVES)
+            first = half * PASSES_IN_HALF
             nc.sync.dma_start(
                 out=w_codes[half][:].bitcast(I32),
-                in_=Wf_words.rearrange("g p n t -> p g (n t)").bitcast(I32)[:, :, cols],
+                in_=Wf_words[first : first + PASSES_IN_HALF].rearrange("g p n t -> p g (n t)").bitcast(I32),
             )
 
         load_scores(0)
         load_auxiliary(0, 0)
         load_auxiliary(0, 1)
         load_target(0)
+        load_scores(1)
         load_weight_scales()
         load_weight_half(0)
-        load_scores(1)
-        load_target(1)
         load_weight_half(1)
+        load_target(1)
         load_scores(2)
         load_auxiliary(1, 0)
         load_auxiliary(1, 1)
@@ -231,7 +231,10 @@ def tile_informationfusion_pb_kernel(tc, scores, auxiliary, target, Wf_words, Wf
                         in_=attn_pairs[:, u * P : (u + 1) * P],
                         identity=ident_f32[:],
                     )
-            nc.scalar.copy(out=attn_grouped[c][:].bitcast(F32), in_=attn_flip[:].rearrange("q u r -> q r u"))
+            nc.scalar.copy(
+                out=attn_grouped[c][:].bitcast(F32).rearrange("q (r i) u -> q r i u", i=TILES),
+                in_=attn_flip[:].rearrange("q u (i r) -> q r i u", i=TILES),
+            )
 
         def quantise_attn(c):
             nc.vector.quantize_mx(
@@ -264,7 +267,10 @@ def tile_informationfusion_pb_kernel(tc, scores, auxiliary, target, Wf_words, Wf
                         in_=target_pairs[:, i, pairs_in_pass * g + u : pairs_in_pass * (g + 1) : PAIRS],
                         identity=ident_f32[:],
                     )
-            nc.scalar.copy(out=x_grouped[(c, g)][:].bitcast(F32), in_=target_flip[:].rearrange("p u r -> p r u"))
+            nc.scalar.copy(
+                out=x_grouped[(c, g)][:].bitcast(F32).rearrange("p (r i) u -> p r i u", i=TILES),
+                in_=target_flip[:].rearrange("p u (i r) -> p r i u", i=TILES),
+            )
 
         def quantise_x(c, g):
             nc.vector.quantize_mx(
@@ -295,13 +301,12 @@ def tile_informationfusion_pb_kernel(tc, scores, auxiliary, target, Wf_words, Wf
 
         def fuse(c, m, passes):
             cols = slice(m * P, (m + 1) * P)
-            half_cols = slice((m % TILES_IN_HALF) * P, (m % TILES_IN_HALF + 1) * P)
             for g in passes:
                 if g == 0:
                     y_acc[(c, m)] = psum_out.tile([P, CHUNK], F32, name="y_acc")
                 nc.tensor.matmul_mx(
                     out=y_acc[(c, m)][:],
-                    lhsT=w_codes[m // TILES_IN_HALF][:, g, half_cols].bitcast(FP8X4),
+                    lhsT=w_codes[g // PASSES_IN_HALF][:, g % PASSES_IN_HALF, cols].bitcast(FP8X4),
                     lhsT_scale=w_planes[SCALE_ROWS * g : P, cols],
                     rhs=x_codes[(c, g)][:].bitcast(FP8X4),
                     rhs_scale=x_scales[(c, g)][:],
@@ -342,14 +347,14 @@ def tile_informationfusion_pb_kernel(tc, scores, auxiliary, target, Wf_words, Wf
         bias_flip = psum_front.tile([P, P], BF16, tag="front")
         nc.tensor.transpose(out=bias_flip[:], in_=bias_rows[:], identity=ident_bf16[:])
         bias_col = const.tile([P, OUT_TILES], F32)
+        nc.scalar.copy(out=bias_col[:], in_=bias_flip[:, 0:OUT_TILES])
         quantise_aux(0, 0)
         regroup_aux(0, 1)
         quantise_attn(0)
         quantise_aux(0, 1)
+        row_max(1)
         for g in target_passes:
             quantise_x(0, g)
-        nc.vector.tensor_copy(out=bias_col[:], in_=bias_flip[:, 0:OUT_TILES])
-        row_max(1)
         for h in range(AUX_PASSES):
             for i in range(TILES):
                 pool(0, h, i)
@@ -369,6 +374,9 @@ def tile_informationfusion_pb_kernel(tc, scores, auxiliary, target, Wf_words, Wf
                 fuse(c, m, aux_passes)
                 finish(c, m)
             if c == 0:
+                for m in late_tiles[:2]:
+                    fuse(c, m, all_passes)
+                    finish(c, m)
                 flip(1)
             if nxt < CHUNKS:
                 quantise_attn(nxt)
@@ -378,9 +386,10 @@ def tile_informationfusion_pb_kernel(tc, scores, auxiliary, target, Wf_words, Wf
                 exponentials(far)
             if c < AUX_PASSES:
                 regroup_aux(1, c)
-            for m in late_tiles[:2]:
-                fuse(c, m, all_passes)
-                finish(c, m)
+            if c > 0:
+                for m in late_tiles[:2]:
+                    fuse(c, m, all_passes)
+                    finish(c, m)
             if far >= CHUNKS and nxt < CHUNKS:
                 for h in range(AUX_PASSES):
                     for i in range(TILES):

@@ -60,8 +60,8 @@ def tile_informationfusion_pb_kernel(tc, scores, auxiliary, target, Wf_words, Wf
         psum_out = ctx.enter_context(tc.psum_pool(name="psum_out", bufs=OUT_BANKS))
 
         bias_rows = const.tile([P, P], BF16)
-        nc.gpsimd.memset(bias_rows[:], 0.0)
-        nc.gpsimd.dma_start(out=bias_rows[0:OUT_TILES, :], in_=b_f.rearrange("(m p) -> m p", p=P))
+        nc.vector.memset(bias_rows[:], 0.0)
+        nc.scalar.dma_start(out=bias_rows[0:OUT_TILES, :], in_=b_f.rearrange("(m p) -> m p", p=P))
         ident_f32 = const.tile([P, P], F32)
         make_identity(nc, ident_f32[:])
         ident_bf16 = const.tile([P, P], BF16)
@@ -370,45 +370,31 @@ def tile_informationfusion_pb_kernel(tc, scores, auxiliary, target, Wf_words, Wf
                 fuse(c, m, target_passes)
             if far < CHUNKS:
                 row_max(far)
-            for m in early_tiles:
-                fuse(c, m, aux_passes)
-                finish(c, m)
-            if c == 0:
-                for m in late_tiles[:2]:
-                    fuse(c, m, all_passes)
-                    finish(c, m)
-                flip(1)
-            if nxt < CHUNKS:
-                quantise_attn(nxt)
-                for g in target_passes:
-                    quantise_x(nxt, g)
-            if far < CHUNKS:
-                exponentials(far)
-            if c < AUX_PASSES:
-                regroup_aux(1, c)
-            if c > 0:
-                for m in late_tiles[:2]:
-                    fuse(c, m, all_passes)
-                    finish(c, m)
-            if far >= CHUNKS and nxt < CHUNKS:
-                for h in range(AUX_PASSES):
-                    for i in range(TILES):
-                        pool(nxt, h, i)
-                for g in aux_passes:
-                    quantise_x(nxt, g)
-            for m in late_tiles[2:]:
-                fuse(c, m, all_passes)
-                finish(c, m)
             if c == 1:
+                regroup_aux(1, 1)
                 quantise_aux(1, 0)
-                quantise_aux(1, 1)
-            if far < CHUNKS:
-                normalise(far)
-            if far < CHUNKS:
-                for h in range(AUX_PASSES):
-                    for i in range(TILES):
-                        pool(nxt, h, i)
-                for g in aux_passes:
-                    quantise_x(nxt, g)
-            if far < CHUNKS:
-                flip(far)
+            for m in range(OUT_TILES):
+                fuse(c, m, aux_passes if m in early_tiles else all_passes)
+                finish(c, m)
+                if nxt < CHUNKS:
+                    if m == 1:
+                        flip_attn(nxt)
+                        flip_target(nxt, 0)
+                        quantise_attn(nxt)
+                        quantise_x(nxt, 0)
+                    if m == 3:
+                        flip_target(nxt, 1)
+                        quantise_x(nxt, 1)
+                        if c == 0:
+                            regroup_aux(1, 0)
+                        if c == 1:
+                            quantise_aux(1, 1)
+                        if far < CHUNKS:
+                            exponentials(far)
+                            normalise(far)
+                    if m == 6:
+                        for h in range(AUX_PASSES):
+                            for i in range(TILES):
+                                pool(nxt, h, i)
+                        for g in aux_passes:
+                            quantise_x(nxt, g)

@@ -35,7 +35,7 @@ AUX_PASSES = DA // K_PASS
 PASSES = TARGET_PASSES + AUX_PASSES
 OUT_TILES = DT // P
 WEIGHT_HALVES = 2
-PASSES_IN_HALF = PASSES // WEIGHT_HALVES
+TILES_IN_HALF = OUT_TILES // WEIGHT_HALVES
 STORE_TILES = 2
 FRONT_BANKS = 4
 OUT_BANKS = 4
@@ -87,7 +87,7 @@ def tile_informationfusion_pb_kernel(tc, scores, auxiliary, target, Wf_words, Wf
                 aux_raw[(b, h)] = per_half.tile([P, PACK, K_PASS], BF16, name="aux_raw")
         w_codes = []
         for half in range(WEIGHT_HALVES):
-            w_tile = per_weight_half.tile([P, PASSES_IN_HALF, DT], U32, align_bytes=64)
+            w_tile = per_weight_half.tile([P, PASSES, DT // WEIGHT_HALVES], U32, align_bytes=64)
             w_codes.append(w_tile)
 
         def chunk_rows(c):
@@ -121,10 +121,10 @@ def tile_informationfusion_pb_kernel(tc, scores, auxiliary, target, Wf_words, Wf
                 )
 
         def load_weight_half(half):
-            first = half * PASSES_IN_HALF
+            cols = slice(half * DT // WEIGHT_HALVES, (half + 1) * DT // WEIGHT_HALVES)
             nc.sync.dma_start(
                 out=w_codes[half][:].bitcast(I32),
-                in_=Wf_words[first : first + PASSES_IN_HALF].rearrange("g p n t -> p g (n t)").bitcast(I32),
+                in_=Wf_words.rearrange("g p n t -> p g (n t)").bitcast(I32)[:, :, cols],
             )
 
         load_scores(0)
@@ -134,8 +134,8 @@ def tile_informationfusion_pb_kernel(tc, scores, auxiliary, target, Wf_words, Wf
         load_scores(1)
         load_weight_scales()
         load_weight_half(0)
-        load_weight_half(1)
         load_target(1)
+        load_weight_half(1)
         load_scores(2)
         load_auxiliary(1, 0)
         load_auxiliary(1, 1)
@@ -243,10 +243,10 @@ def tile_informationfusion_pb_kernel(tc, scores, auxiliary, target, Wf_words, Wf
                 in_=attn_grouped[c][:].rearrange("q r j -> q (r j)"),
             )
 
-        def regroup_aux(b, h):
-            nc.vector.tensor_copy(
-                out=aux_grouped[b][:, h].rearrange("q t p j -> q p j t"),
-                in_=aux_raw[(b, h)][:].rearrange("q j (p t) -> q p j t", t=PACK),
+        def regroup_aux(b, h, t_range=slice(0, PACK), copy=nc.vector.tensor_copy):
+            copy(
+                out=aux_grouped[b][:, h, t_range].rearrange("q t p j -> q p j t"),
+                in_=aux_raw[(b, h)][:].rearrange("q j (p t) -> q p j t", t=PACK)[:, :, :, t_range],
             )
 
         def quantise_aux(b, h):
@@ -294,19 +294,20 @@ def tile_informationfusion_pb_kernel(tc, scores, auxiliary, target, Wf_words, Wf
                     stop=True,
                 )
             grouped = x_grouped[(c, TARGET_PASSES + h)][:, rows, :]
-            if h == 0:
+            if h == 0 or (c == 0 and i == 0):
                 nc.scalar.copy(out=grouped, in_=pooled[:].rearrange("p t r -> p r t"))
             else:
                 nc.vector.tensor_copy(out=grouped, in_=pooled[:].rearrange("p t r -> p r t"))
 
         def fuse(c, m, passes):
             cols = slice(m * P, (m + 1) * P)
+            half_cols = slice((m % TILES_IN_HALF) * P, (m % TILES_IN_HALF + 1) * P)
             for g in passes:
                 if g == 0:
                     y_acc[(c, m)] = psum_out.tile([P, CHUNK], F32, name="y_acc")
                 nc.tensor.matmul_mx(
                     out=y_acc[(c, m)][:],
-                    lhsT=w_codes[g // PASSES_IN_HALF][:, g % PASSES_IN_HALF, cols].bitcast(FP8X4),
+                    lhsT=w_codes[m // TILES_IN_HALF][:, g, half_cols].bitcast(FP8X4),
                     lhsT_scale=w_planes[SCALE_ROWS * g : P, cols],
                     rhs=x_codes[(c, g)][:].bitcast(FP8X4),
                     rhs_scale=x_scales[(c, g)][:],
@@ -321,7 +322,11 @@ def tile_informationfusion_pb_kernel(tc, scores, auxiliary, target, Wf_words, Wf
             nc.scalar.activation(
                 out=y_pair[c][:, slot, :], in_=y_acc[(c, m)][:], func=ACT.Tanh, bias=bias_col[:, m : m + 1], scale=1.0
             )
-            if slot == STORE_TILES - 1:
+            if c == CHUNKS - 1 and m >= OUT_TILES - STORE_TILES:
+                nc.sync.dma_start(
+                    out=out[c // CHUNKS_IN_BATCH, m * P : (m + 1) * P, chunk_rows(c)], in_=y_pair[c][:, slot, :]
+                )
+            elif slot == STORE_TILES - 1:
                 features = slice((m + 1 - STORE_TILES) * P, (m + 1) * P)
                 nc.sync.dma_start(
                     out=out[c // CHUNKS_IN_BATCH, features, chunk_rows(c)].rearrange("(s p) r -> p s r", p=P),
@@ -366,6 +371,9 @@ def tile_informationfusion_pb_kernel(tc, scores, auxiliary, target, Wf_words, Wf
         for c in range(CHUNKS):
             nxt = c + 1
             far = c + 2
+            flip_after = 3 if c == 0 else 1
+            flip2_after = 3 if c == 0 else 3
+            pool_after = 6 if c == 0 else 6
             for m in early_tiles:
                 fuse(c, m, target_passes)
             if far < CHUNKS:
@@ -377,12 +385,12 @@ def tile_informationfusion_pb_kernel(tc, scores, auxiliary, target, Wf_words, Wf
                 fuse(c, m, aux_passes if m in early_tiles else all_passes)
                 finish(c, m)
                 if nxt < CHUNKS:
-                    if m == 1:
+                    if m == flip_after:
                         flip_attn(nxt)
                         flip_target(nxt, 0)
                         quantise_attn(nxt)
                         quantise_x(nxt, 0)
-                    if m == 3:
+                    if m == flip2_after:
                         flip_target(nxt, 1)
                         quantise_x(nxt, 1)
                         if c == 0:
@@ -392,7 +400,7 @@ def tile_informationfusion_pb_kernel(tc, scores, auxiliary, target, Wf_words, Wf
                         if far < CHUNKS:
                             exponentials(far)
                             normalise(far)
-                    if m == 6:
+                    if m == pool_after:
                         for h in range(AUX_PASSES):
                             for i in range(TILES):
                                 pool(nxt, h, i)

@@ -34,6 +34,8 @@ TARGET_PASSES = DT // K_PASS
 AUX_PASSES = DA // K_PASS
 PASSES = TARGET_PASSES + AUX_PASSES
 OUT_TILES = DT // P
+WEIGHT_PARTS = 2
+PART_PASSES = PASSES // WEIGHT_PARTS
 WEIGHT_HALVES = 2
 TILES_IN_HALF = OUT_TILES // WEIGHT_HALVES
 STORE_TILES = 2
@@ -51,7 +53,7 @@ def tile_informationfusion_pb_kernel(tc, scores, auxiliary, target, Wf_words, Wf
         per_batch = ctx.enter_context(tc.tile_pool(name="per_batch", bufs=B))
         per_chunk = ctx.enter_context(tc.tile_pool(name="per_chunk", bufs=CHUNKS))
         per_half = ctx.enter_context(tc.tile_pool(name="per_half", bufs=B * AUX_PASSES))
-        per_weight_half = ctx.enter_context(tc.tile_pool(name="per_weight_half", bufs=WEIGHT_HALVES))
+        per_weight = ctx.enter_context(tc.tile_pool(name="per_weight", bufs=WEIGHT_PARTS * WEIGHT_HALVES))
         per_pass = ctx.enter_context(tc.tile_pool(name="per_pass", bufs=CHUNKS * PASSES))
         per_tile = ctx.enter_context(tc.tile_pool(name="per_tile", bufs=CHUNKS * TILES))
         work = ctx.enter_context(tc.tile_pool(name="work", bufs=2 * TILES))
@@ -74,36 +76,39 @@ def tile_informationfusion_pb_kernel(tc, scores, auxiliary, target, Wf_words, Wf
         nc.vector.memset(table_warmer[:], 0.0)
         nc.scalar.activation(out=table_warmer[:], in_=table_warmer[:], func=ACT.Exp)
 
-        scores_sb = []
+        scores_sb = {}
         target_raw = []
         aux_raw = {}
         for c in range(CHUNKS):
-            s_tile = per_chunk.tile([P, TILES, LA], BF16)
-            scores_sb.append(s_tile)
+            for i in range(TILES):
+                scores_sb[(c, i)] = per_tile.tile([P, LA], BF16, name="scores_sb")
             t_tile = per_chunk.tile([P, TILES, DT], BF16)
             target_raw.append(t_tile)
         for b in range(B):
             for h in range(AUX_PASSES):
                 aux_raw[(b, h)] = per_half.tile([P, PACK, K_PASS], BF16, name="aux_raw")
-        w_codes = []
-        for half in range(WEIGHT_HALVES):
-            w_tile = per_weight_half.tile([P, PASSES, DT // WEIGHT_HALVES], U32, align_bytes=64)
-            w_codes.append(w_tile)
+        w_codes = {}
+        for part in range(WEIGHT_PARTS):
+            for half in range(WEIGHT_HALVES):
+                w_codes[(part, half)] = per_weight.tile(
+                    [P, PART_PASSES, DT // WEIGHT_HALVES], U32, align_bytes=64, name="w_codes"
+                )
 
         def chunk_rows(c):
             first = (c % CHUNKS_IN_BATCH) * CHUNK
             return slice(first, first + CHUNK)
 
         def load_scores(c):
-            nc.sync.dma_start(
-                out=scores_sb[c][:],
-                in_=scores[c // CHUNKS_IN_BATCH, chunk_rows(c), :].rearrange("(p i) a -> p i a", i=TILES),
-            )
+            for i in range(TILES):
+                first = (c % CHUNKS_IN_BATCH) * CHUNK + i * P
+                nc.sync.dma_start(
+                    out=scores_sb[(c, i)][:], in_=scores[c // CHUNKS_IN_BATCH, first : first + P, :]
+                )
 
         def load_target(c):
             nc.sync.dma_start(
                 out=target_raw[c][:],
-                in_=target[c // CHUNKS_IN_BATCH, chunk_rows(c), :].rearrange("(p i) k -> p i k", i=TILES),
+                in_=target[c // CHUNKS_IN_BATCH, chunk_rows(c), :].rearrange("(i p) k -> p i k", p=P),
             )
 
         def load_auxiliary(b, h):
@@ -120,11 +125,12 @@ def tile_informationfusion_pb_kernel(tc, scores, auxiliary, target, Wf_words, Wf
                     in_=Wf_scales[:, SCALE_ROWS * quad : SCALE_ROWS * (quad + 1), :].bitcast(I32),
                 )
 
-        def load_weight_half(half):
+        def load_weights(part, half):
             cols = slice(half * DT // WEIGHT_HALVES, (half + 1) * DT // WEIGHT_HALVES)
+            passes = slice(part * PART_PASSES, (part + 1) * PART_PASSES)
             nc.sync.dma_start(
-                out=w_codes[half][:].bitcast(I32),
-                in_=Wf_words.rearrange("g p n t -> p g (n t)").bitcast(I32)[:, :, cols],
+                out=w_codes[(part, half)][:].bitcast(I32),
+                in_=Wf_words.rearrange("g p n t -> p g (n t)").bitcast(I32)[:, passes, cols],
             )
 
         load_scores(0)
@@ -133,9 +139,11 @@ def tile_informationfusion_pb_kernel(tc, scores, auxiliary, target, Wf_words, Wf
         load_target(0)
         load_scores(1)
         load_weight_scales()
-        load_weight_half(0)
+        load_weights(0, 0)
         load_target(1)
-        load_weight_half(1)
+        load_weights(1, 0)
+        load_weights(0, 1)
+        load_weights(1, 1)
         load_scores(2)
         load_auxiliary(1, 0)
         load_auxiliary(1, 1)
@@ -187,7 +195,7 @@ def tile_informationfusion_pb_kernel(tc, scores, auxiliary, target, Wf_words, Wf
                 neg_max[(c, i)] = per_tile.tile([P, 1], F32, name="neg_max")
                 nc.vector.tensor_scalar(
                     out=negated[:],
-                    in0=scores_sb[c][:, i, :],
+                    in0=scores_sb[(c, i)][:],
                     scalar1=-1.0,
                     scalar2=None,
                     op0=ALU.mult,
@@ -201,16 +209,17 @@ def tile_informationfusion_pb_kernel(tc, scores, auxiliary, target, Wf_words, Wf
                 exp_sorted[(c, i)] = work.tile([P, PAIRS, P, PAIR], F32, name="exp_sorted")
                 nc.scalar.activation(
                     out=exp_sorted[(c, i)][:].rearrange("p u q e -> p q u e"),
-                    in_=scores_sb[c][:, i, :].rearrange("p (q u e) -> p q u e", u=PAIRS, e=PAIR),
+                    in_=scores_sb[(c, i)][:].rearrange("p (q u e) -> p q u e", u=PAIRS, e=PAIR),
                     func=ACT.Exp,
                     bias=neg_max[(c, i)][:],
                     scale=1.0,
                     accum_out=row_sum[c][:, i : i + 1],
                 )
 
-        def normalise(c):
+        def normalise(c, each=False):
             inv_sum = per_chunk.tile([P, TILES], F32)
-            nc.vector.reciprocal(out=inv_sum[:], in_=row_sum[c][:])
+            for i in range(TILES):
+                nc.vector.reciprocal(out=inv_sum[:, i : i + 1], in_=row_sum[c][:, i : i + 1])
             for i in range(TILES):
                 attn_sorted[(c, i)] = work.tile([P, LA], BF16, name="attn_sorted")
                 nc.vector.tensor_scalar(
@@ -221,7 +230,7 @@ def tile_informationfusion_pb_kernel(tc, scores, auxiliary, target, Wf_words, Wf
                     op0=ALU.mult,
                 )
 
-        def flip_attn(c):
+        def flip_attn(c, copy=nc.scalar.copy):
             attn_flip = psum_front.tile([P, PAIRS, CHUNK], F32, tag="front")
             for i in range(TILES):
                 attn_pairs = attn_sorted[(c, i)][:].bitcast(F32)
@@ -231,10 +240,7 @@ def tile_informationfusion_pb_kernel(tc, scores, auxiliary, target, Wf_words, Wf
                         in_=attn_pairs[:, u * P : (u + 1) * P],
                         identity=ident_f32[:],
                     )
-            nc.scalar.copy(
-                out=attn_grouped[c][:].bitcast(F32).rearrange("q (r i) u -> q r i u", i=TILES),
-                in_=attn_flip[:].rearrange("q u (i r) -> q r i u", i=TILES),
-            )
+            copy(out=attn_grouped[c][:].bitcast(F32), in_=attn_flip[:].rearrange("q u r -> q r u"))
 
         def quantise_attn(c):
             nc.vector.quantize_mx(
@@ -243,10 +249,10 @@ def tile_informationfusion_pb_kernel(tc, scores, auxiliary, target, Wf_words, Wf
                 in_=attn_grouped[c][:].rearrange("q r j -> q (r j)"),
             )
 
-        def regroup_aux(b, h, t_range=slice(0, PACK), copy=nc.vector.tensor_copy):
+        def regroup_aux(b, h, words=slice(0, P), copy=nc.vector.tensor_copy):
             copy(
-                out=aux_grouped[b][:, h, t_range].rearrange("q t p j -> q p j t"),
-                in_=aux_raw[(b, h)][:].rearrange("q j (p t) -> q p j t", t=PACK)[:, :, :, t_range],
+                out=aux_grouped[b][:, h, :, words, :].rearrange("q t p j -> q p j t"),
+                in_=aux_raw[(b, h)][:].rearrange("q j (p t) -> q p j t", t=PACK)[:, words, :, :],
             )
 
         def quantise_aux(b, h):
@@ -256,7 +262,7 @@ def tile_informationfusion_pb_kernel(tc, scores, auxiliary, target, Wf_words, Wf
                 in_=aux_grouped[b][:, h].rearrange("q t p j -> q (t p j)"),
             )
 
-        def flip_target(c, g):
+        def flip_target(c, g, copy=nc.scalar.copy):
             pairs_in_pass = P * PAIRS
             target_pairs = target_raw[c][:].bitcast(F32)
             target_flip = psum_front.tile([P, PAIRS, CHUNK], F32, tag="front")
@@ -267,10 +273,7 @@ def tile_informationfusion_pb_kernel(tc, scores, auxiliary, target, Wf_words, Wf
                         in_=target_pairs[:, i, pairs_in_pass * g + u : pairs_in_pass * (g + 1) : PAIRS],
                         identity=ident_f32[:],
                     )
-            nc.scalar.copy(
-                out=x_grouped[(c, g)][:].bitcast(F32).rearrange("p (r i) u -> p r i u", i=TILES),
-                in_=target_flip[:].rearrange("p u (i r) -> p r i u", i=TILES),
-            )
+            copy(out=x_grouped[(c, g)][:].bitcast(F32), in_=target_flip[:].rearrange("p u r -> p r u"))
 
         def quantise_x(c, g):
             nc.vector.quantize_mx(
@@ -279,7 +282,7 @@ def tile_informationfusion_pb_kernel(tc, scores, auxiliary, target, Wf_words, Wf
                 in_=x_grouped[(c, g)][:].rearrange("p r t -> p (r t)"),
             )
 
-        def pool(c, h, i):
+        def pool(c, h, i, copy):
             b = c // CHUNKS_IN_BATCH
             rows = slice(i * P, (i + 1) * P)
             pooled = psum_front.tile([P, PACK, P], F32, tag="front")
@@ -294,20 +297,20 @@ def tile_informationfusion_pb_kernel(tc, scores, auxiliary, target, Wf_words, Wf
                     stop=True,
                 )
             grouped = x_grouped[(c, TARGET_PASSES + h)][:, rows, :]
-            if h == 0 or (c == 0 and i == 0):
-                nc.scalar.copy(out=grouped, in_=pooled[:].rearrange("p t r -> p r t"))
-            else:
-                nc.vector.tensor_copy(out=grouped, in_=pooled[:].rearrange("p t r -> p r t"))
+            copy(out=grouped, in_=pooled[:].rearrange("p t r -> p r t"))
 
         def fuse(c, m, passes):
             cols = slice(m * P, (m + 1) * P)
             half_cols = slice((m % TILES_IN_HALF) * P, (m % TILES_IN_HALF + 1) * P)
             for g in passes:
                 if g == 0:
-                    y_acc[(c, m)] = psum_out.tile([P, CHUNK], F32, name="y_acc")
+                    if c == CHUNKS - 1 and m not in early_tiles:
+                        y_acc[(c, m)] = psum_front.tile([P, CHUNK], F32, tag="front", name="y_acc")
+                    else:
+                        y_acc[(c, m)] = psum_out.tile([P, CHUNK], F32, name="y_acc")
                 nc.tensor.matmul_mx(
                     out=y_acc[(c, m)][:],
-                    lhsT=w_codes[m // TILES_IN_HALF][:, g, half_cols].bitcast(FP8X4),
+                    lhsT=w_codes[(g // PART_PASSES, m // TILES_IN_HALF)][:, g % PART_PASSES, half_cols].bitcast(FP8X4),
                     lhsT_scale=w_planes[SCALE_ROWS * g : P, cols],
                     rhs=x_codes[(c, g)][:].bitcast(FP8X4),
                     rhs_scale=x_scales[(c, g)][:],
@@ -336,73 +339,86 @@ def tile_informationfusion_pb_kernel(tc, scores, auxiliary, target, Wf_words, Wf
         target_passes = range(TARGET_PASSES)
         aux_passes = range(TARGET_PASSES, PASSES)
         all_passes = range(PASSES)
-        early_tiles = range(OUT_BANKS)
-        late_tiles = range(OUT_BANKS, OUT_TILES)
+        early_tiles = range(4)
+        on_scalar = nc.scalar.copy
+        on_vector = nc.vector.tensor_copy
 
-        def flip(c):
-            flip_attn(c)
-            for g in target_passes:
-                flip_target(c, g)
+        def pools(c, h, copies):
+            for i in range(TILES):
+                pool(c, h, i, copies[i])
 
         row_max(0)
         exponentials(0)
-        regroup_aux(0, 0)
+        regroup_aux(0, 0, slice(0, 64))
         normalise(0)
-        flip(0)
+        regroup_aux(0, 0, slice(64, 128))
+        regroup_aux(0, 1, slice(64, 128), on_scalar)
+        flip_attn(0)
+        flip_target(0, 0)
+        flip_target(0, 1)
         bias_flip = psum_front.tile([P, P], BF16, tag="front")
         nc.tensor.transpose(out=bias_flip[:], in_=bias_rows[:], identity=ident_bf16[:])
         bias_col = const.tile([P, OUT_TILES], F32)
         nc.scalar.copy(out=bias_col[:], in_=bias_flip[:, 0:OUT_TILES])
+        regroup_aux(0, 1, slice(0, 64))
         quantise_aux(0, 0)
-        regroup_aux(0, 1)
         quantise_attn(0)
+        pool(0, 0, 0, on_scalar)
+        pool(0, 0, 1, on_scalar)
         quantise_aux(0, 1)
+        quantise_x(0,0)
         row_max(1)
-        for g in target_passes:
-            quantise_x(0, g)
-        for h in range(AUX_PASSES):
-            for i in range(TILES):
-                pool(0, h, i)
         exponentials(1)
-        for g in aux_passes:
-            quantise_x(0, g)
+        quantise_x(0,1)
+        pool(0, 1, 0, on_vector)
+        pool(0, 1, 1, on_vector)
+        for m in early_tiles:
+            fuse(0, m, target_passes)
+        quantise_x(0,2)
+        quantise_x(0,3)
+        flip_target(1, 0)
+        flip_target(1, 1)
         normalise(1)
+        quantise_x(1,0)
+        quantise_x(1,1)
 
         for c in range(CHUNKS):
             nxt = c + 1
             far = c + 2
-            flip_after = 3 if c == 0 else 1
-            flip2_after = 3 if c == 0 else 3
-            pool_after = 6 if c == 0 else 6
-            for m in early_tiles:
-                fuse(c, m, target_passes)
+            if c > 0:
+                for m in early_tiles:
+                    fuse(c, m, target_passes)
             if far < CHUNKS:
                 row_max(far)
             if c == 1:
-                regroup_aux(1, 1)
+                regroup_aux(1, 1, slice(64, P), on_scalar)
+                regroup_aux(1, 1, slice(0, 64))
                 quantise_aux(1, 0)
             for m in range(OUT_TILES):
                 fuse(c, m, aux_passes if m in early_tiles else all_passes)
                 finish(c, m)
                 if nxt < CHUNKS:
-                    if m == flip_after:
+                    if m == (1, 1, 1)[c]:
                         flip_attn(nxt)
-                        flip_target(nxt, 0)
                         quantise_attn(nxt)
+                    if m == (9, 1, 1)[c]:
+                        flip_target(nxt, 0)
                         quantise_x(nxt, 0)
-                    if m == flip2_after:
+                    if m == (9, 3, 3)[c]:
                         flip_target(nxt, 1)
                         quantise_x(nxt, 1)
-                        if c == 0:
-                            regroup_aux(1, 0)
-                        if c == 1:
-                            quantise_aux(1, 1)
-                        if far < CHUNKS:
-                            exponentials(far)
-                            normalise(far)
-                    if m == pool_after:
-                        for h in range(AUX_PASSES):
-                            for i in range(TILES):
-                                pool(nxt, h, i)
+                    if m == 3 and c == 0:
+                        regroup_aux(1, 0)
+                    if m == 2 and c == 1:
+                        quantise_aux(1, 1)
+                    if m == (3, 3, 3)[c] and far < CHUNKS:
+                        exponentials(far)
+                    if m == (6, 6, 6)[c] and far < CHUNKS:
+                        normalise(far)
+                    if m == (5, 5, 5)[c]:
+                        pool(nxt, 0, 0, on_scalar)
+                        pool(nxt, 0, 1, on_vector)
+                        pool(nxt, 1, 0, on_scalar)
+                        pool(nxt, 1, 1, on_vector)
                         for g in aux_passes:
                             quantise_x(nxt, g)

@@ -262,15 +262,27 @@ def tile_informationfusion_pb_kernel(tc, scores, auxiliary, target, Wf_words, Wf
                 in_=aux_grouped[b][:, h].rearrange("q t p j -> q (t p j)"),
             )
 
+        target_sorted = {}
+
+        def sort_target(c):
+            target_sorted[c] = per_chunk.tile([P, TILES, TARGET_PASSES, PAIRS, P], F32, name="target_sorted")
+            for i in range(TILES):
+                nc.vector.tensor_copy(
+                    out=target_sorted[c][:, i],
+                    in_=target_raw[c][:, i, :].bitcast(F32).rearrange("p (g q u) -> p g u q", g=TARGET_PASSES, u=PAIRS),
+                )
+
         def flip_target(c, g, copy=nc.scalar.copy):
-            pairs_in_pass = P * PAIRS
-            target_pairs = target_raw[c][:].bitcast(F32)
+            if c in target_sorted:
+                pairs = target_sorted[c][:, :, g]
+            else:
+                pairs = target_raw[c][:].bitcast(F32).rearrange("p i (g q u) -> p i g u q", g=TARGET_PASSES, u=PAIRS)[:, :, g]
             target_flip = psum_front.tile([P, PAIRS, CHUNK], F32, tag="front")
             for u in range(PAIRS):
                 for i in range(TILES):
                     nc.tensor.transpose(
                         out=target_flip[:, u, i * P : (i + 1) * P],
-                        in_=target_pairs[:, i, pairs_in_pass * g + u : pairs_in_pass * (g + 1) : PAIRS],
+                        in_=pairs[:, i, u, :],
                         identity=ident_f32[:],
                     )
             copy(out=x_grouped[(c, g)][:].bitcast(F32), in_=target_flip[:].rearrange("p u r -> p r u"))
@@ -339,7 +351,7 @@ def tile_informationfusion_pb_kernel(tc, scores, auxiliary, target, Wf_words, Wf
         target_passes = range(TARGET_PASSES)
         aux_passes = range(TARGET_PASSES, PASSES)
         all_passes = range(PASSES)
-        early_tiles = range(4)
+        early_tiles = range(3)
         on_scalar = nc.scalar.copy
         on_vector = nc.vector.tensor_copy
 
@@ -376,11 +388,13 @@ def tile_informationfusion_pb_kernel(tc, scores, auxiliary, target, Wf_words, Wf
             fuse(0, m, target_passes)
         quantise_x(0,2)
         quantise_x(0,3)
+        normalise(1)
         flip_target(1, 0)
         flip_target(1, 1)
-        normalise(1)
+        flip_attn(1)
         quantise_x(1,0)
         quantise_x(1,1)
+        quantise_attn(1)
 
         for c in range(CHUNKS):
             nxt = c + 1
@@ -388,8 +402,6 @@ def tile_informationfusion_pb_kernel(tc, scores, auxiliary, target, Wf_words, Wf
             if c > 0:
                 for m in early_tiles:
                     fuse(c, m, target_passes)
-            if far < CHUNKS:
-                row_max(far)
             if c == 1:
                 regroup_aux(1, 1, slice(64, P), on_scalar)
                 regroup_aux(1, 1, slice(0, 64))
@@ -398,21 +410,28 @@ def tile_informationfusion_pb_kernel(tc, scores, auxiliary, target, Wf_words, Wf
                 fuse(c, m, aux_passes if m in early_tiles else all_passes)
                 finish(c, m)
                 if nxt < CHUNKS:
-                    if m == (1, 1, 1)[c]:
+                    if m == (9,1,1)[c]:
                         flip_attn(nxt)
-                        quantise_attn(nxt)
                     if m == (9, 1, 1)[c]:
                         flip_target(nxt, 0)
-                        quantise_x(nxt, 0)
-                    if m == (9, 3, 3)[c]:
+                    if m == (9,1,1)[c]:
                         flip_target(nxt, 1)
+                    if m == (9,1,1)[c]:
+                        quantise_attn(nxt)
+                    if m == (9, 1, 1)[c]:
+                        quantise_x(nxt, 0)
+                    if m == (9,1,1)[c]:
                         quantise_x(nxt, 1)
+                    if m == (1,0,0)[c] and far < CHUNKS:
+                        row_max(far)
                     if m == 3 and c == 0:
                         regroup_aux(1, 0)
                     if m == 2 and c == 1:
                         quantise_aux(1, 1)
                     if m == (3, 3, 3)[c] and far < CHUNKS:
                         exponentials(far)
+                    if m == (7,7,7)[c] and far < CHUNKS:
+                        sort_target(far)
                     if m == (6, 6, 6)[c] and far < CHUNKS:
                         normalise(far)
                     if m == (5, 5, 5)[c]:

@@ -63,7 +63,6 @@ def tile_informationfusion_pb_kernel(tc, scores, auxiliary, target, Wf_words, Wf
 
         bias_rows = const.tile([P, P], BF16)
         nc.vector.memset(bias_rows[:], 0.0)
-        nc.scalar.dma_start(out=bias_rows[0:OUT_TILES, :], in_=b_f.rearrange("(m p) -> m p", p=P))
         ident_f32 = const.tile([P, P], F32)
         make_identity(nc, ident_f32[:])
         ident_bf16 = const.tile([P, P], BF16)
@@ -134,6 +133,7 @@ def tile_informationfusion_pb_kernel(tc, scores, auxiliary, target, Wf_words, Wf
             )
 
         load_scores(0)
+        nc.sync.dma_start(out=bias_rows[0:OUT_TILES, :], in_=b_f.rearrange("(m p) -> m p", p=P))
         load_auxiliary(0, 0)
         load_auxiliary(0, 1)
         load_target(0)
@@ -216,16 +216,19 @@ def tile_informationfusion_pb_kernel(tc, scores, auxiliary, target, Wf_words, Wf
                     accum_out=row_sum[c][:, i : i + 1],
                 )
 
-        def normalise(c, each=False):
-            inv_sum = per_chunk.tile([P, TILES], F32)
-            for i in range(TILES):
-                nc.vector.reciprocal(out=inv_sum[:, i : i + 1], in_=row_sum[c][:, i : i + 1])
+        inv_sum = {}
+
+        def reciprocals(c):
+            inv_sum[c] = per_chunk.tile([P, TILES], F32, name="inv_sum")
+            nc.vector.reciprocal(out=inv_sum[c][:], in_=row_sum[c][:])
+
+        def normalise(c):
             for i in range(TILES):
                 attn_sorted[(c, i)] = work.tile([P, LA], BF16, name="attn_sorted")
                 nc.vector.tensor_scalar(
                     out=attn_sorted[(c, i)][:],
                     in0=exp_sorted[(c, i)][:].rearrange("p u q e -> p (u q e)"),
-                    scalar1=inv_sum[:, i : i + 1],
+                    scalar1=inv_sum[c][:, i : i + 1],
                     scalar2=None,
                     op0=ALU.mult,
                 )
@@ -249,10 +252,10 @@ def tile_informationfusion_pb_kernel(tc, scores, auxiliary, target, Wf_words, Wf
                 in_=attn_grouped[c][:].rearrange("q r j -> q (r j)"),
             )
 
-        def regroup_aux(b, h, words=slice(0, P), copy=nc.vector.tensor_copy):
+        def regroup_aux(b, h, t_range=slice(0, PACK), copy=nc.vector.tensor_copy):
             copy(
-                out=aux_grouped[b][:, h, :, words, :].rearrange("q t p j -> q p j t"),
-                in_=aux_raw[(b, h)][:].rearrange("q j (p t) -> q p j t", t=PACK)[:, words, :, :],
+                out=aux_grouped[b][:, h, t_range].rearrange("q t p j -> q p j t"),
+                in_=aux_raw[(b, h)][:].rearrange("q j (p t) -> q p j t", t=PACK)[:, :, :, t_range],
             )
 
         def quantise_aux(b, h):
@@ -330,6 +333,31 @@ def tile_informationfusion_pb_kernel(tc, scores, auxiliary, target, Wf_words, Wf
                     stop=(g == PASSES - 1),
                 )
 
+        def close_last(c, m):
+            cols = slice(m * P, (m + 1) * P)
+            half_cols = slice((m % TILES_IN_HALF) * P, (m % TILES_IN_HALF + 1) * P)
+            for i in range(TILES):
+                rows = slice(i * P, (i + 1) * P)
+                last_acc = psum_front.tile([P, P], F32, tag="front")
+                for g in all_passes:
+                    nc.tensor.matmul_mx(
+                        out=last_acc[:],
+                        lhsT=w_codes[(g // PART_PASSES, m // TILES_IN_HALF)][:, g % PART_PASSES, half_cols].bitcast(FP8X4),
+                        lhsT_scale=w_planes[SCALE_ROWS * g : P, cols],
+                        rhs=x_codes[(c, g)][:, rows].bitcast(FP8X4),
+                        rhs_scale=x_scales[(c, g)][:, rows],
+                        start=(g == 0),
+                        stop=(g == PASSES - 1),
+                    )
+                y_last = per_tile.tile([P, P], F32)
+                nc.scalar.activation(
+                    out=y_last[:], in_=last_acc[:], func=ACT.Tanh, bias=bias_col[:, m : m + 1], scale=1.0
+                )
+                first = (c % CHUNKS_IN_BATCH) * CHUNK + i * P
+                nc.sync.dma_start(
+                    out=out[c // CHUNKS_IN_BATCH, m * P : (m + 1) * P, first : first + P], in_=y_last[:]
+                )
+
         def finish(c, m):
             slot = m % STORE_TILES
             if slot == 0:
@@ -351,20 +379,17 @@ def tile_informationfusion_pb_kernel(tc, scores, auxiliary, target, Wf_words, Wf
         target_passes = range(TARGET_PASSES)
         aux_passes = range(TARGET_PASSES, PASSES)
         all_passes = range(PASSES)
-        early_tiles = range(3)
+        early_tiles = range(4)
         on_scalar = nc.scalar.copy
         on_vector = nc.vector.tensor_copy
 
-        def pools(c, h, copies):
-            for i in range(TILES):
-                pool(c, h, i, copies[i])
-
         row_max(0)
         exponentials(0)
-        regroup_aux(0, 0, slice(0, 64))
+        regroup_aux(0, 0, slice(0, 2))
+        reciprocals(0)
         normalise(0)
-        regroup_aux(0, 0, slice(64, 128))
-        regroup_aux(0, 1, slice(64, 128), on_scalar)
+        regroup_aux(0, 0, slice(2, 4))
+        regroup_aux(0, 1, slice(2, 4), on_scalar)
         flip_attn(0)
         flip_target(0, 0)
         flip_target(0, 1)
@@ -372,7 +397,7 @@ def tile_informationfusion_pb_kernel(tc, scores, auxiliary, target, Wf_words, Wf
         nc.tensor.transpose(out=bias_flip[:], in_=bias_rows[:], identity=ident_bf16[:])
         bias_col = const.tile([P, OUT_TILES], F32)
         nc.scalar.copy(out=bias_col[:], in_=bias_flip[:, 0:OUT_TILES])
-        regroup_aux(0, 1, slice(0, 64))
+        regroup_aux(0, 1, slice(0, 2))
         quantise_aux(0, 0)
         quantise_attn(0)
         pool(0, 0, 0, on_scalar)
@@ -387,14 +412,13 @@ def tile_informationfusion_pb_kernel(tc, scores, auxiliary, target, Wf_words, Wf
         for m in early_tiles:
             fuse(0, m, target_passes)
         quantise_x(0,2)
+        reciprocals(1)
         quantise_x(0,3)
-        normalise(1)
         flip_target(1, 0)
         flip_target(1, 1)
-        flip_attn(1)
+        normalise(1)
         quantise_x(1,0)
         quantise_x(1,1)
-        quantise_attn(1)
 
         for c in range(CHUNKS):
             nxt = c + 1
@@ -403,41 +427,46 @@ def tile_informationfusion_pb_kernel(tc, scores, auxiliary, target, Wf_words, Wf
                 for m in early_tiles:
                     fuse(c, m, target_passes)
             if c == 1:
-                regroup_aux(1, 1, slice(64, P), on_scalar)
-                regroup_aux(1, 1, slice(0, 64))
+                regroup_aux(1, 1, slice(2, PACK), on_scalar)
+                regroup_aux(1, 1, slice(0, 2))
                 quantise_aux(1, 0)
             for m in range(OUT_TILES):
+                if c == CHUNKS - 1 and m == OUT_TILES - 1:
+                    close_last(c, m)
+                    continue
                 fuse(c, m, aux_passes if m in early_tiles else all_passes)
                 finish(c, m)
                 if nxt < CHUNKS:
-                    if m == (9,1,1)[c]:
+                    if m == (1,2,2)[c]:
                         flip_attn(nxt)
-                    if m == (9, 1, 1)[c]:
+                    if m == (9,2,2)[c]:
                         flip_target(nxt, 0)
-                    if m == (9,1,1)[c]:
+                    if m == (9,2,2)[c]:
                         flip_target(nxt, 1)
-                    if m == (9,1,1)[c]:
+                    if m == (1,2,2)[c]:
                         quantise_attn(nxt)
-                    if m == (9, 1, 1)[c]:
+                    if m == (9,2,2)[c]:
                         quantise_x(nxt, 0)
-                    if m == (9,1,1)[c]:
+                    if m == (9,2,2)[c]:
                         quantise_x(nxt, 1)
-                    if m == (1,0,0)[c] and far < CHUNKS:
+                    if m == (0,0,0)[c] and far < CHUNKS:
                         row_max(far)
                     if m == 3 and c == 0:
                         regroup_aux(1, 0)
-                    if m == 2 and c == 1:
+                    if m == 1 and c == 1:
                         quantise_aux(1, 1)
                     if m == (3, 3, 3)[c] and far < CHUNKS:
                         exponentials(far)
-                    if m == (7,7,7)[c] and far < CHUNKS:
+                    if m == (9,5,5)[c] and far < CHUNKS:
                         sort_target(far)
                     if m == (6, 6, 6)[c] and far < CHUNKS:
                         normalise(far)
                     if m == (5, 5, 5)[c]:
-                        pool(nxt, 0, 0, on_scalar)
+                        pool(nxt, 0, 0, on_vector)
                         pool(nxt, 0, 1, on_vector)
                         pool(nxt, 1, 0, on_scalar)
                         pool(nxt, 1, 1, on_vector)
-                        for g in aux_passes:
-                            quantise_x(nxt, g)
+                        quantise_x(nxt, 2)
+                        if far < CHUNKS:
+                            reciprocals(far)
+                        quantise_x(nxt, 3)

from contextlib import ExitStack

import concourse.mybir as mybir
from concourse.masks import make_identity

F32 = mybir.dt.float32
BF16 = mybir.dt.bfloat16
I32 = mybir.dt.int32
U32 = mybir.dt.uint32
U8 = mybir.dt.uint8
FP8X4 = mybir.dt.float8_e4m3fn_x4
ACT = mybir.ActivationFunctionType
ALU = mybir.AluOpType

P = 128
PACK = 4
K_PASS = P * PACK
PAIRS = 2
PAIR = 2
QUADRANTS = 4
QUADRANT = P // QUADRANTS
SCALE_ROWS = 4

B = 2
LT = 512
LA = 512
DT = 1024
DA = 1024
CHUNK = 256
TILES = CHUNK // P
CHUNKS_IN_BATCH = LT // CHUNK
CHUNKS = B * CHUNKS_IN_BATCH
TARGET_PASSES = DT // K_PASS
AUX_PASSES = DA // K_PASS
PASSES = TARGET_PASSES + AUX_PASSES
OUT_TILES = DT // P
WEIGHT_PARTS = 2
PART_PASSES = PASSES // WEIGHT_PARTS
WEIGHT_HALVES = 2
TILES_IN_HALF = OUT_TILES // WEIGHT_HALVES
STORE_TILES = 2
FRONT_BANKS = 4
OUT_BANKS = 4

FLOPS = 2 * B * LT * LA * DA + 2 * B * LT * (DT + DA) * DT


def tile_informationfusion_pb_kernel(tc, scores, auxiliary, target, Wf_words, Wf_scales, b_f, out):
    nc = tc.nc
    with ExitStack() as ctx:
        ctx.enter_context(tc.manual_schedule())
        const = ctx.enter_context(tc.tile_pool(name="const", bufs=1))
        per_batch = ctx.enter_context(tc.tile_pool(name="per_batch", bufs=B))
        per_chunk = ctx.enter_context(tc.tile_pool(name="per_chunk", bufs=CHUNKS))
        per_half = ctx.enter_context(tc.tile_pool(name="per_half", bufs=B * AUX_PASSES))
        per_weight = ctx.enter_context(tc.tile_pool(name="per_weight", bufs=WEIGHT_PARTS * WEIGHT_HALVES))
        per_pass = ctx.enter_context(tc.tile_pool(name="per_pass", bufs=CHUNKS * PASSES))
        per_tile = ctx.enter_context(tc.tile_pool(name="per_tile", bufs=CHUNKS * TILES))
        work = ctx.enter_context(tc.tile_pool(name="work", bufs=2 * TILES))
        results = ctx.enter_context(tc.tile_pool(name="results", bufs=OUT_TILES))
        psum_front = ctx.enter_context(tc.psum_pool(name="psum_front", bufs=FRONT_BANKS))
        psum_out = ctx.enter_context(tc.psum_pool(name="psum_out", bufs=OUT_BANKS))

        bias_rows = const.tile([P, P], BF16)
        nc.vector.memset(bias_rows[:], 0.0)
        ident_f32 = const.tile([P, P], F32)
        make_identity(nc, ident_f32[:])
        ident_bf16 = const.tile([P, P], BF16)
        make_identity(nc, ident_bf16[:])

        w_planes = const.tile([P, DT], U8, align_bytes=64)
        nc.vector.memset(w_planes[:].bitcast(I32), 0)

        table_warmer = const.tile([P, 1], F32)
        nc.vector.memset(table_warmer[:], 0.0)
        nc.scalar.activation(out=table_warmer[:], in_=table_warmer[:], func=ACT.Exp)

        scores_sb = {}
        target_raw = []
        aux_raw = {}
        for c in range(CHUNKS):
            for i in range(TILES):
                scores_sb[(c, i)] = per_tile.tile([P, LA], BF16, name="scores_sb")
            t_tile = per_chunk.tile([P, TILES, DT], BF16)
            target_raw.append(t_tile)
        for b in range(B):
            for h in range(AUX_PASSES):
                aux_raw[(b, h)] = per_half.tile([P, PACK, K_PASS], BF16, name="aux_raw")
        w_codes = {}
        for part in range(WEIGHT_PARTS):
            for half in range(WEIGHT_HALVES):
                w_codes[(part, half)] = per_weight.tile(
                    [P, PART_PASSES, DT // WEIGHT_HALVES], U32, align_bytes=64, name="w_codes"
                )

        def chunk_rows(c):
            first = (c % CHUNKS_IN_BATCH) * CHUNK
            return slice(first, first + CHUNK)

        def load_scores(c):
            for i in range(TILES):
                first = (c % CHUNKS_IN_BATCH) * CHUNK + i * P
                nc.sync.dma_start(
                    out=scores_sb[(c, i)][:], in_=scores[c // CHUNKS_IN_BATCH, first : first + P, :]
                )

        def load_target(c):
            nc.sync.dma_start(
                out=target_raw[c][:],
                in_=target[c // CHUNKS_IN_BATCH, chunk_rows(c), :].rearrange("(i p) k -> p i k", p=P),
            )

        def load_auxiliary(b, h):
            cols = slice(h * K_PASS, (h + 1) * K_PASS)
            nc.sync.dma_start(
                out=aux_raw[(b, h)][:], in_=auxiliary[b].rearrange("(q j) d -> q j d", j=PACK)[:, :, cols]
            )

        def load_weight_scales():
            for quad in range(QUADRANTS):
                first = QUADRANT * quad
                nc.sync.dma_start(
                    out=w_planes[first : first + PASSES * SCALE_ROWS, :].bitcast(I32),
                    in_=Wf_scales[:, SCALE_ROWS * quad : SCALE_ROWS * (quad + 1), :].bitcast(I32),
                )

        def load_weights(part, half):
            cols = slice(half * DT // WEIGHT_HALVES, (half + 1) * DT // WEIGHT_HALVES)
            passes = slice(part * PART_PASSES, (part + 1) * PART_PASSES)
            nc.sync.dma_start(
                out=w_codes[(part, half)][:].bitcast(I32),
                in_=Wf_words.rearrange("g p n t -> p g (n t)").bitcast(I32)[:, passes, cols],
            )

        load_scores(0)
        nc.sync.dma_start(out=bias_rows[0:OUT_TILES, :], in_=b_f.rearrange("(m p) -> m p", p=P))
        load_auxiliary(0, 0)
        load_auxiliary(0, 1)
        load_target(0)
        load_scores(1)
        load_weight_scales()
        load_weights(0, 0)
        load_target(1)
        load_weights(1, 0)
        load_weights(0, 1)
        load_weights(1, 1)
        load_scores(2)
        load_auxiliary(1, 0)
        load_auxiliary(1, 1)
        load_target(2)
        load_scores(3)
        load_target(3)

        attn_grouped = []
        attn_codes = []
        attn_scales = []
        x_grouped = {}
        x_codes = {}
        x_scales = {}
        for c in range(CHUNKS):
            at_grouped = per_chunk.tile([P, CHUNK, PACK], BF16, align_bytes=64)
            at_codes = per_chunk.tile([P, CHUNK], U32, align_bytes=64)
            at_scales = per_chunk.tile([P, CHUNK], U8, align_bytes=64)
            attn_grouped.append(at_grouped)
            attn_codes.append(at_codes)
            attn_scales.append(at_scales)
            for g in range(PASSES):
                xg_tile = per_pass.tile([P, CHUNK, PACK], BF16, align_bytes=64)
                xc_tile = per_pass.tile([P, CHUNK], U32, align_bytes=64)
                xs_tile = per_pass.tile([P, CHUNK], U8, align_bytes=64)
                x_grouped[(c, g)] = xg_tile
                x_codes[(c, g)] = xc_tile
                x_scales[(c, g)] = xs_tile
        aux_grouped = []
        aux_codes = []
        aux_scales = []
        for b in range(B):
            ax_grouped = per_batch.tile([P, AUX_PASSES, PACK, P, PACK], BF16, align_bytes=64)
            ax_codes = per_batch.tile([P, AUX_PASSES, PACK, P], U32, align_bytes=64)
            ax_scales = per_batch.tile([P, AUX_PASSES, PACK, P], U8, align_bytes=64)
            aux_grouped.append(ax_grouped)
            aux_codes.append(ax_codes)
            aux_scales.append(ax_scales)

        neg_max = {}
        row_sum = {}
        exp_sorted = {}
        attn_sorted = {}
        y_acc = {}
        y_pair = {}

        def row_max(c):
            for i in range(TILES):
                negated = work.tile([P, LA], BF16)
                neg_max[(c, i)] = per_tile.tile([P, 1], F32, name="neg_max")
                nc.vector.tensor_scalar(
                    out=negated[:],
                    in0=scores_sb[(c, i)][:],
                    scalar1=-1.0,
                    scalar2=None,
                    op0=ALU.mult,
                    op1=ALU.min,
                    accum_out=neg_max[(c, i)][:],
                )

        def exponentials(c):
            row_sum[c] = per_chunk.tile([P, TILES], F32, name="row_sum")
            for i in range(TILES):
                exp_sorted[(c, i)] = work.tile([P, PAIRS, P, PAIR], F32, name="exp_sorted")
                nc.scalar.activation(
                    out=exp_sorted[(c, i)][:].rearrange("p u q e -> p q u e"),
                    in_=scores_sb[(c, i)][:].rearrange("p (q u e) -> p q u e", u=PAIRS, e=PAIR),
                    func=ACT.Exp,
                    bias=neg_max[(c, i)][:],
                    scale=1.0,
                    accum_out=row_sum[c][:, i : i + 1],
                )

        inv_sum = {}

        def reciprocals(c):
            inv_sum[c] = per_chunk.tile([P, TILES], F32, name="inv_sum")
            nc.vector.reciprocal(out=inv_sum[c][:], in_=row_sum[c][:])

        def normalise(c):
            for i in range(TILES):
                attn_sorted[(c, i)] = work.tile([P, LA], BF16, name="attn_sorted")
                nc.vector.tensor_scalar(
                    out=attn_sorted[(c, i)][:],
                    in0=exp_sorted[(c, i)][:].rearrange("p u q e -> p (u q e)"),
                    scalar1=inv_sum[c][:, i : i + 1],
                    scalar2=None,
                    op0=ALU.mult,
                )

        def flip_attn(c, copy=nc.scalar.copy):
            attn_flip = psum_front.tile([P, PAIRS, CHUNK], F32, tag="front")
            for i in range(TILES):
                attn_pairs = attn_sorted[(c, i)][:].bitcast(F32)
                for u in range(PAIRS):
                    nc.tensor.transpose(
                        out=attn_flip[:, u, i * P : (i + 1) * P],
                        in_=attn_pairs[:, u * P : (u + 1) * P],
                        identity=ident_f32[:],
                    )
            copy(out=attn_grouped[c][:].bitcast(F32), in_=attn_flip[:].rearrange("q u r -> q r u"))

        def quantise_attn(c):
            nc.vector.quantize_mx(
                out=attn_codes[c][:].bitcast(FP8X4),
                scales=attn_scales[c][:],
                in_=attn_grouped[c][:].rearrange("q r j -> q (r j)"),
            )

        def regroup_aux(b, h, t_range=slice(0, PACK), copy=nc.vector.tensor_copy):
            copy(
                out=aux_grouped[b][:, h, t_range].rearrange("q t p j -> q p j t"),
                in_=aux_raw[(b, h)][:].rearrange("q j (p t) -> q p j t", t=PACK)[:, :, :, t_range],
            )

        def quantise_aux(b, h):
            nc.vector.quantize_mx(
                out=aux_codes[b][:, h].rearrange("q t p -> q (t p)").bitcast(FP8X4),
                scales=aux_scales[b][:, h].rearrange("q t p -> q (t p)"),
                in_=aux_grouped[b][:, h].rearrange("q t p j -> q (t p j)"),
            )

        target_sorted = {}

        def sort_target(c):
            target_sorted[c] = per_chunk.tile([P, TILES, TARGET_PASSES, PAIRS, P], F32, name="target_sorted")
            for i in range(TILES):
                nc.vector.tensor_copy(
                    out=target_sorted[c][:, i],
                    in_=target_raw[c][:, i, :].bitcast(F32).rearrange("p (g q u) -> p g u q", g=TARGET_PASSES, u=PAIRS),
                )

        def flip_target(c, g, copy=nc.scalar.copy):
            if c in target_sorted:
                pairs = target_sorted[c][:, :, g]
            else:
                pairs = target_raw[c][:].bitcast(F32).rearrange("p i (g q u) -> p i g u q", g=TARGET_PASSES, u=PAIRS)[:, :, g]
            target_flip = psum_front.tile([P, PAIRS, CHUNK], F32, tag="front")
            for u in range(PAIRS):
                for i in range(TILES):
                    nc.tensor.transpose(
                        out=target_flip[:, u, i * P : (i + 1) * P],
                        in_=pairs[:, i, u, :],
                        identity=ident_f32[:],
                    )
            copy(out=x_grouped[(c, g)][:].bitcast(F32), in_=target_flip[:].rearrange("p u r -> p r u"))

        def quantise_x(c, g):
            nc.vector.quantize_mx(
                out=x_codes[(c, g)][:].bitcast(FP8X4),
                scales=x_scales[(c, g)][:],
                in_=x_grouped[(c, g)][:].rearrange("p r t -> p (r t)"),
            )

        def pool(c, h, i, copy):
            b = c // CHUNKS_IN_BATCH
            rows = slice(i * P, (i + 1) * P)
            pooled = psum_front.tile([P, PACK, P], F32, tag="front")
            for t in range(PACK):
                nc.tensor.matmul_mx(
                    out=pooled[:, t, :],
                    lhsT=aux_codes[b][:, h, t, :].bitcast(FP8X4),
                    lhsT_scale=aux_scales[b][:, h, t, :],
                    rhs=attn_codes[c][:, rows].bitcast(FP8X4),
                    rhs_scale=attn_scales[c][:, rows],
                    start=True,
                    stop=True,
                )
            grouped = x_grouped[(c, TARGET_PASSES + h)][:, rows, :]
            copy(out=grouped, in_=pooled[:].rearrange("p t r -> p r t"))

        def fuse(c, m, passes):
            cols = slice(m * P, (m + 1) * P)
            half_cols = slice((m % TILES_IN_HALF) * P, (m % TILES_IN_HALF + 1) * P)
            for g in passes:
                if g == 0:
                    if c == CHUNKS - 1 and m not in early_tiles:
                        y_acc[(c, m)] = psum_front.tile([P, CHUNK], F32, tag="front", name="y_acc")
                    else:
                        y_acc[(c, m)] = psum_out.tile([P, CHUNK], F32, name="y_acc")
                nc.tensor.matmul_mx(
                    out=y_acc[(c, m)][:],
                    lhsT=w_codes[(g // PART_PASSES, m // TILES_IN_HALF)][:, g % PART_PASSES, half_cols].bitcast(FP8X4),
                    lhsT_scale=w_planes[SCALE_ROWS * g : P, cols],
                    rhs=x_codes[(c, g)][:].bitcast(FP8X4),
                    rhs_scale=x_scales[(c, g)][:],
                    start=(g == 0),
                    stop=(g == PASSES - 1),
                )

        def close_last(c, m):
            cols = slice(m * P, (m + 1) * P)
            half_cols = slice((m % TILES_IN_HALF) * P, (m % TILES_IN_HALF + 1) * P)
            for i in range(TILES):
                rows = slice(i * P, (i + 1) * P)
                last_acc = psum_front.tile([P, P], F32, tag="front")
                for g in all_passes:
                    nc.tensor.matmul_mx(
                        out=last_acc[:],
                        lhsT=w_codes[(g // PART_PASSES, m // TILES_IN_HALF)][:, g % PART_PASSES, half_cols].bitcast(FP8X4),
                        lhsT_scale=w_planes[SCALE_ROWS * g : P, cols],
                        rhs=x_codes[(c, g)][:, rows].bitcast(FP8X4),
                        rhs_scale=x_scales[(c, g)][:, rows],
                        start=(g == 0),
                        stop=(g == PASSES - 1),
                    )
                y_last = per_tile.tile([P, P], F32)
                nc.scalar.activation(
                    out=y_last[:], in_=last_acc[:], func=ACT.Tanh, bias=bias_col[:, m : m + 1], scale=1.0
                )
                first = (c % CHUNKS_IN_BATCH) * CHUNK + i * P
                nc.sync.dma_start(
                    out=out[c // CHUNKS_IN_BATCH, m * P : (m + 1) * P, first : first + P], in_=y_last[:]
                )

        def finish(c, m):
            slot = m % STORE_TILES
            if slot == 0:
                y_pair[c] = results.tile([P, STORE_TILES, CHUNK], F32, name="y_pair")
            nc.scalar.activation(
                out=y_pair[c][:, slot, :], in_=y_acc[(c, m)][:], func=ACT.Tanh, bias=bias_col[:, m : m + 1], scale=1.0
            )
            if c == CHUNKS - 1 and m >= OUT_TILES - STORE_TILES:
                nc.sync.dma_start(
                    out=out[c // CHUNKS_IN_BATCH, m * P : (m + 1) * P, chunk_rows(c)], in_=y_pair[c][:, slot, :]
                )
            elif slot == STORE_TILES - 1:
                features = slice((m + 1 - STORE_TILES) * P, (m + 1) * P)
                nc.sync.dma_start(
                    out=out[c // CHUNKS_IN_BATCH, features, chunk_rows(c)].rearrange("(s p) r -> p s r", p=P),
                    in_=y_pair[c][:],
                )

        target_passes = range(TARGET_PASSES)
        aux_passes = range(TARGET_PASSES, PASSES)
        all_passes = range(PASSES)
        early_tiles = range(4)
        on_scalar = nc.scalar.copy
        on_vector = nc.vector.tensor_copy

        row_max(0)
        exponentials(0)
        regroup_aux(0, 0, slice(0, 2))
        reciprocals(0)
        normalise(0)
        regroup_aux(0, 0, slice(2, 4))
        regroup_aux(0, 1, slice(2, 4), on_scalar)
        flip_attn(0)
        flip_target(0, 0)
        flip_target(0, 1)
        bias_flip = psum_front.tile([P, P], BF16, tag="front")
        nc.tensor.transpose(out=bias_flip[:], in_=bias_rows[:], identity=ident_bf16[:])
        bias_col = const.tile([P, OUT_TILES], F32)
        nc.scalar.copy(out=bias_col[:], in_=bias_flip[:, 0:OUT_TILES])
        regroup_aux(0, 1, slice(0, 2))
        quantise_aux(0, 0)
        quantise_attn(0)
        pool(0, 0, 0, on_scalar)
        pool(0, 0, 1, on_scalar)
        quantise_aux(0, 1)
        quantise_x(0,0)
        row_max(1)
        exponentials(1)
        quantise_x(0,1)
        pool(0, 1, 0, on_vector)
        pool(0, 1, 1, on_vector)
        for m in early_tiles:
            fuse(0, m, target_passes)
        quantise_x(0,2)
        reciprocals(1)
        quantise_x(0,3)
        flip_target(1, 0)
        flip_target(1, 1)
        normalise(1)
        quantise_x(1,0)
        quantise_x(1,1)

        for c in range(CHUNKS):
            nxt = c + 1
            far = c + 2
            if c > 0:
                for m in early_tiles:
                    fuse(c, m, target_passes)
            if c == 1:
                regroup_aux(1, 1, slice(2, PACK), on_scalar)
                regroup_aux(1, 1, slice(0, 2))
                quantise_aux(1, 0)
            for m in range(OUT_TILES):
                if c == CHUNKS - 1 and m == OUT_TILES - 1:
                    close_last(c, m)
                    continue
                fuse(c, m, aux_passes if m in early_tiles else all_passes)
                finish(c, m)
                if nxt < CHUNKS:
                    if m == (1,2,2)[c]:
                        flip_attn(nxt)
                    if m == (9,2,2)[c]:
                        flip_target(nxt, 0)
                    if m == (9,2,2)[c]:
                        flip_target(nxt, 1)
                    if m == (1,2,2)[c]:
                        quantise_attn(nxt)
                    if m == (9,2,2)[c]:
                        quantise_x(nxt, 0)
                    if m == (9,2,2)[c]:
                        quantise_x(nxt, 1)
                    if m == (0,0,0)[c] and far < CHUNKS:
                        row_max(far)
                    if m == 3 and c == 0:
                        regroup_aux(1, 0)
                    if m == 1 and c == 1:
                        quantise_aux(1, 1)
                    if m == (3, 3, 3)[c] and far < CHUNKS:
                        exponentials(far)
                    if m == (9,5,5)[c] and far < CHUNKS:
                        sort_target(far)
                    if m == (6, 6, 6)[c] and far < CHUNKS:
                        normalise(far)
                    if m == (5, 5, 5)[c]:
                        pool(nxt, 0, 0, on_vector)
                        pool(nxt, 0, 1, on_vector)
                        pool(nxt, 1, 0, on_scalar)
                        pool(nxt, 1, 1, on_vector)
                        quantise_x(nxt, 2)
                        if far < CHUNKS:
                            reciprocals(far)
                        quantise_x(nxt, 3)
